import numpy as np
import ml_dtypes


def mxq(x, axis, fmt="e4m3"):
    dtype, down = {"e4m3": (ml_dtypes.float8_e4m3fn, 7), "e5m2": (ml_dtypes.float8_e5m2, 14)}[fmt]
    v = np.moveaxis(np.asarray(x, np.float32).astype(ml_dtypes.bfloat16).astype(np.float64), axis, -1)
    blocks = v.reshape(v.shape[:-1] + (-1, 32))
    amax = np.abs(blocks).max(-1, keepdims=True)
    byte = np.maximum(np.where(amax > 0, np.frexp(amax)[1] - 1 + 127, 0) - down, 1)
    scale = np.exp2(byte - 127.0)
    codes = (blocks / scale).astype(np.float32).astype(dtype).astype(np.float64)
    return np.moveaxis((codes * scale).reshape(v.shape), -1, axis)


WIDE = False


def mx_kscale(k):
    if not WIDE:
        return np.ones(k)
    levels = np.array([10, -10, 5, -5, 0])
    a = np.random.permutation(np.resize(levels, k // 512 * 4)).reshape(k // 512, 4)
    idx = np.arange(k)
    return np.exp2(a[idx // 512, idx % 128 // 32])


BF16 = ml_dtypes.bfloat16


def bf(x):
    return np.asarray(x, np.float32).astype(BF16)


def f64(x):
    return np.asarray(x).astype(np.float64)


E2M1 = np.array([0.0, 0.5, 1.0, 1.5, 2.0, 3.0, 4.0, 6.0, -0.0, -0.5, -1.0, -1.5, -2.0, -3.0, -4.0, -6.0])


def pack_weight(w, fmt):
    k, n = w.shape
    w = f64(bf(w)).reshape(k // 32, 32, n)
    amax = np.abs(w).max(1)
    if fmt == "e4m3":
        byte = np.frexp(amax)[1] - 1 + 127 - 7
    else:
        mant, ex = np.frexp(amax / 6.0)
        byte = np.where(mant > 0.5, ex, ex - 1) + 127
    byte = np.clip(np.where(amax > 0, byte, 1), 1, 254)
    scaled = (w * np.exp2(127.0 - byte)[:, None, :]).reshape(k, n).astype(np.float32)
    by_word = np.ascontiguousarray(scaled.reshape(k // 512, 128, 4, n).transpose(0, 1, 3, 2))
    if fmt == "e4m3":
        words = by_word.astype(ml_dtypes.float8_e4m3fn).view(np.uint8)
    else:
        c = by_word.astype(ml_dtypes.float4_e2m1fn).view(np.uint8) & 0xF
        words = c[..., 0::2] | (c[..., 1::2] << 4)
    return np.ascontiguousarray(words), np.ascontiguousarray(byte.astype(np.uint8).reshape(k // 512, 16, n))


def unpack_weight(words, scales, fmt):
    g, p, n, _ = words.shape
    if fmt == "e4m3":
        vals = np.ascontiguousarray(words).view(ml_dtypes.float8_e4m3fn).astype(np.float64)
    else:
        nib = np.empty((g, p, n, 4), np.uint8)
        nib[..., 0::2] = words & 0xF
        nib[..., 1::2] = words >> 4
        vals = E2M1[nib]
    vals = vals * np.repeat(np.exp2(scales.astype(np.float64) - 127.0), 8, axis=1)[..., None]
    return vals.transpose(0, 1, 3, 2).reshape(g * 512, n)


B, D, H, O = 128, 3072, 3072, 3072


def silu(v):
    with np.errstate(over="ignore"):
        return v / (1.0 + np.exp(-v))


def setup_inputs():
    s = mx_kscale(H)
    u = s / s.min()
    t = bf(np.random.random(B))
    W1_words, W1_scales = pack_weight(np.ascontiguousarray((np.random.standard_normal((H, D)) * 2.0 / np.sqrt(D) * u[:, None]).T), "e4m3")
    b1 = bf(np.random.standard_normal(H) * 0.5 * u)
    W2_words, W2_scales = pack_weight(np.ascontiguousarray((np.random.standard_normal((O, H)) * 1.5 / np.sqrt(H) / u[None, :]).T), "e4m3")
    b2 = bf(np.random.standard_normal(O) * 0.5)
    return {"t": t,
            "W1_words": W1_words,
            "W1_scales": W1_scales,
            "b1": b1,
            "W2_words": W2_words,
            "W2_scales": W2_scales,
            "b2": b2}


def reference(t, W1_words, W1_scales, b1, W2_words, W2_scales, b2):
    t = f64(t)
    phase = (np.arange(D, dtype=np.float64) / D) * np.pi
    tb = t[:, None]
    emb = tb * np.cos(phase[None, :] * tb) + tb * np.sin(phase[None, :] * (1.0 - tb))
    x = silu((mxq(emb, 1, "e4m3") @ unpack_weight(W1_words, W1_scales, "e4m3")) + f64(b1))
    x = silu((mxq(x, 1, "e4m3") @ unpack_weight(W2_words, W2_scales, "e4m3")) + f64(b2))
    return x

@@ -1,0 +1,186 @@
+import math
+from contextlib import ExitStack
+
+import concourse.mybir as mybir
+from concourse.masks import make_identity
+
+F32 = mybir.dt.float32
+BF16 = mybir.dt.bfloat16
+I32 = mybir.dt.int32
+U32 = mybir.dt.uint32
+U8 = mybir.dt.uint8
+FP8X4 = mybir.dt.float8_e4m3fn_x4
+ALU = mybir.AluOpType
+ACT = mybir.ActivationFunctionType
+
+P = 128
+WIDTH = 3072
+GROUPS = 6
+NT = 512
+BANKS = 6
+FLOPS = 2 * 2 * 128 * 3072 * 3072
+
+
+def w1_plane(g):
+    return (0, 4 * g) if g < 4 else (1, 4 * (g - 4))
+
+
+def w2_plane(g):
+    return (1, 8 + 4 * g) if g < 2 else (2, 4 * (g - 2))
+
+
+def tile_input_timestep_w_kernel(tc, t, W1_words, W1_scales, b1, W2_words, W2_scales, b2, out):
+    nc = tc.nc
+    with ExitStack() as ctx:
+        ctx.enter_context(tc.manual_schedule())
+        const = ctx.enter_context(tc.tile_pool(name="const", bufs=1))
+        wpool = ctx.enter_context(tc.tile_pool(name="weights", bufs=1))
+        work = ctx.enter_context(tc.tile_pool(name="work", bufs=2))
+        accp = ctx.enter_context(tc.psum_pool(name="acc", bufs=1))
+        auxp = ctx.enter_context(tc.psum_pool(name="aux", bufs=2))
+
+        planes = [const.tile([P, WIDTH], U8, name="plane%d" % i, align_bytes=64) for i in range(3)]
+        rows = const.tile([P, NT], BF16, name="rows")
+        ident_b = const.tile([P, P], BF16, name="ident_b")
+        ident_f = const.tile([P, P], F32, name="ident_f")
+        idx = const.tile([P, 4 * GROUPS], I32, name="idx")
+        idxf = const.tile([P, 4 * GROUPS], F32, name="idxf")
+        hphi = const.tile([P, 4 * GROUPS], F32, name="hphi")
+        cfac = const.tile([P, 4 * GROUPS], F32, name="cfac")
+        warm = const.tile([P, 1], F32, name="warm")
+        u = const.tile([P, P], F32, name="u")
+        t2 = const.tile([P, P], F32, name="t2")
+        b1s = const.tile([P, GROUPS, 4, P], BF16, name="b1s")
+        b2b = const.tile([P, WIDTH], BF16, name="b2b")
+        embq = const.tile([P, GROUPS, P], U32, name="embq", align_bytes=64)
+        embs = const.tile([P, GROUPS, P], U8, name="embs", align_bytes=64)
+        hq = const.tile([P, GROUPS, P], U32, name="hq", align_bytes=64)
+        hs = const.tile([P, GROUPS, P], U8, name="hs", align_bytes=64)
+        w1 = [wpool.tile([P, WIDTH], U32, name="w1_%d" % g, align_bytes=64) for g in range(GROUPS)]
+        w2 = [wpool.tile([P, WIDTH], U32, name="w2_%d" % g, align_bytes=64) for g in range(GROUPS - 1)]
+        w2last = [wpool.tile([P, NT], U32, name="w2l_%d" % c, align_bytes=64) for c in range(BANKS)]
+
+        nc.vector.memset(planes[0][:].bitcast(I32), 0)
+        nc.vector.memset(rows[:], 0.0)
+        nc.vector.memset(planes[1][:].bitcast(I32), 0)
+        nc.vector.memset(planes[2][:].bitcast(I32), 0)
+
+        nc.scalar.dma_start(out=rows[12:13, 0:P], in_=t.rearrange("(o n) -> o n", o=1))
+        nc.scalar.dma_start(out=rows[0:6, :], in_=b1.rearrange("(c n) -> c n", c=6))
+        nc.scalar.dma_start(out=rows[6:12, :], in_=b2.rearrange("(c n) -> c n", c=6))
+
+        for q in range(4):
+            nc.sync.dma_start(out=planes[0][32 * q:32 * q + 16, :].bitcast(I32),
+                              in_=W1_scales[0:4, 4 * q:4 * q + 4, :].bitcast(I32))
+        for q in range(4):
+            nc.sync.dma_start(out=planes[1][32 * q:32 * q + 8, :].bitcast(I32),
+                              in_=W1_scales[4:6, 4 * q:4 * q + 4, :].bitcast(I32))
+        for q in range(4):
+            nc.sync.dma_start(out=planes[1][32 * q + 8:32 * q + 16, :].bitcast(I32),
+                              in_=W2_scales[0:2, 4 * q:4 * q + 4, :].bitcast(I32))
+        for q in range(4):
+            nc.sync.dma_start(out=planes[2][32 * q:32 * q + 16, :].bitcast(I32),
+                              in_=W2_scales[2:6, 4 * q:4 * q + 4, :].bitcast(I32))
+        for g in range(GROUPS):
+            nc.sync.dma_start(out=w1[g][:].bitcast(I32),
+                              in_=W1_words[g].rearrange("p n t -> p (n t)").bitcast(I32))
+        for g in range(GROUPS - 1):
+            nc.sync.dma_start(out=w2[g][:].bitcast(I32),
+                              in_=W2_words[g].rearrange("p n t -> p (n t)").bitcast(I32))
+        for c in range(BANKS):
+            nc.sync.dma_start(out=w2last[c][:].bitcast(I32),
+                              in_=W2_words[GROUPS - 1].rearrange("p n t -> p (n t)")[:, 4 * NT * c:4 * NT * (c + 1)].bitcast(I32))
+
+        make_identity(nc, ident_b[:])
+        nc.gpsimd.iota(idx[:], pattern=[[NT, GROUPS], [1, 4]], base=0, channel_multiplier=4)
+        make_identity(nc, ident_f[:])
+
+        def spread_row(r):
+            ps = auxp.tile([P, NT], F32, name="aux")
+            nc.tensor.matmul(ps[:], lhsT=ident_b[:, r:r + 1].to_broadcast([P, P]), rhs=rows[:], start=True, stop=True)
+            return ps
+
+        nc.vector.tensor_copy(out=idxf[:], in_=idx[:])
+        nc.vector.tensor_scalar_mul(out=hphi[:], in0=idxf[:], scalar1=math.pi / (2 * WIDTH))
+        nc.scalar.activation(out=cfac[:], in_=hphi[:], func=ACT.Sin, bias=math.pi / 4, scale=1.0)
+
+        tb = spread_row(12)
+        nc.vector.tensor_scalar(out=u[:], in0=tb[:, 0:P], scalar1=-2.0, scalar2=1.0, op0=ALU.mult, op1=ALU.add)
+        nc.vector.tensor_scalar_mul(out=t2[:], in0=tb[:, 0:P], scalar1=2.0)
+
+        xs = {}
+        cts = {}
+        egs = {}
+        for step in range(GROUPS + 2):
+            if step < GROUPS:
+                g = step
+                x = work.tile([P, P, 4], F32, name="x")
+                nc.vector.tensor_tensor(out=x[:], in0=hphi[:, 4 * g:4 * g + 4].unsqueeze(1).to_broadcast([P, P, 4]),
+                                        in1=u[:].unsqueeze(2).to_broadcast([P, P, 4]), op=ALU.mult)
+                nc.scalar.activation(out=x[:], in_=x[:], func=ACT.Sin, bias=math.pi / 4, scale=1.0)
+                ct = work.tile([P, P, 4], F32, name="ct")
+                nc.vector.tensor_tensor(out=ct[:], in0=cfac[:, 4 * g:4 * g + 4].unsqueeze(1).to_broadcast([P, P, 4]),
+                                        in1=t2[:].unsqueeze(2).to_broadcast([P, P, 4]), op=ALU.mult)
+                xs[g] = x
+                cts[g] = ct
+                ps = spread_row(g)
+                nc.scalar.copy(out=b1s[:, g], in_=ps[:].rearrange("p (q t) -> p t q", t=4))
+            if 1 <= step <= GROUPS:
+                g = step - 1
+                eg = work.tile([P, P, 4], BF16, name="eg", align_bytes=64)
+                nc.vector.tensor_tensor(out=eg[:], in0=xs[g][:], in1=cts[g][:], op=ALU.mult)
+                egs[g] = eg
+            if step >= 2:
+                g = step - 2
+                nc.vector.quantize_mx(out=embq[:, g, :].bitcast(FP8X4), scales=embs[:, g, :],
+                                      in_=egs[g][:].rearrange("p b j -> p (b j)"))
+        nc.scalar.activation(out=warm[:], in_=hphi[:, 0:1], func=ACT.Silu)
+
+        acc1 = [accp.tile([P, NT], F32, name="acc%d" % c) for c in range(BANKS)]
+        for g in range(GROUPS):
+            pi, k = w1_plane(g)
+            for c in range(BANKS):
+                cols = slice(c * NT, (c + 1) * NT)
+                nc.tensor.matmul_mx(out=acc1[c][:], lhsT=embq[:, g, :].bitcast(FP8X4), lhsT_scale=embs[:, g, :],
+                                    rhs=w1[g][:, cols].bitcast(FP8X4), rhs_scale=planes[pi][k:P, cols],
+                                    start=(g == 0), stop=(g == GROUPS - 1))
+            ps = spread_row(6 + g)
+            nc.scalar.copy(out=b2b[:, g * NT:(g + 1) * NT], in_=ps[:])
+
+        hgs = {}
+        for step in range(GROUPS + 2):
+            if step < GROUPS:
+                c = step
+                z = work.tile([P, 4, P], F32, name="z", bufs=3)
+                nc.vector.tensor_tensor(out=z[:], in0=acc1[c][:].rearrange("p (q t) -> p t q", t=4), in1=b1s[:, c], op=ALU.add)
+                xt = auxp.tile([P, NT], F32, name="aux")
+                for j in range(4):
+                    nc.tensor.transpose(xt[:, j * P:(j + 1) * P], z[:, j, :], ident_f[:])
+                hg = work.tile([P, P, 4], BF16, name="hg", bufs=3, align_bytes=64)
+                nc.scalar.activation(out=hg[:], in_=xt[:].rearrange("p (t r) -> p r t", t=4), func=ACT.Silu)
+                hgs[c] = hg
+            if step >= 2:
+                c = step - 2
+                nc.vector.quantize_mx(out=hq[:, c, :].bitcast(FP8X4), scales=hs[:, c, :],
+                                      in_=hgs[c][:].rearrange("p b j -> p (b j)"))
+
+        acc2 = [accp.tile([P, NT], F32, name="acc%d" % c) for c in range(BANKS)]
+        for g in range(GROUPS - 1):
+            pi, k = w2_plane(g)
+            for c in range(BANKS):
+                cols = slice(c * NT, (c + 1) * NT)
+                nc.tensor.matmul_mx(out=acc2[c][:], lhsT=hq[:, g, :].bitcast(FP8X4), lhsT_scale=hs[:, g, :],
+                                    rhs=w2[g][:, cols].bitcast(FP8X4), rhs_scale=planes[pi][k:P, cols],
+                                    start=(g == 0), stop=False)
+        g = GROUPS - 1
+        pi, k = w2_plane(g)
+        for c in range(BANKS):
+            cols = slice(c * NT, (c + 1) * NT)
+            nc.tensor.matmul_mx(out=acc2[c][:], lhsT=hq[:, g, :].bitcast(FP8X4), lhsT_scale=hs[:, g, :],
+                                rhs=w2last[c][:].bitcast(FP8X4), rhs_scale=planes[pi][k:P, cols],
+                                start=False, stop=True)
+            z2 = work.tile([P, NT], F32, name="z2", bufs=3)
+            nc.vector.tensor_tensor(out=z2[:], in0=acc2[c][:], in1=b2b[:, cols], op=ALU.add)
+            o = work.tile([P, NT], F32, name="o", bufs=6)
+            nc.scalar.activation(out=o[:], in_=z2[:], func=ACT.Silu)
+            nc.sync.dma_start(out=out[:, cols], in_=o[:])

@@ -26,7 +26,7 @@ def w1_plane(g):
 
 
 def w2_plane(g):
-    return (1, 8 + 4 * g) if g < 2 else (2, 4 * (g - 2))
+    return (2, 4 * g) if g < 4 else (3, 4 * (g - 4))
 
 
 def tile_input_timestep_w_kernel(tc, t, W1_words, W1_scales, b1, W2_words, W2_scales, b2, out):
@@ -39,7 +39,7 @@ def tile_input_timestep_w_kernel(tc, t, W1_words, W1_scales, b1, W2_words, W2_sc
         accp = ctx.enter_context(tc.psum_pool(name="acc", bufs=1))
         auxp = ctx.enter_context(tc.psum_pool(name="aux", bufs=2))
 
-        planes = [const.tile([P, WIDTH], U8, name="plane%d" % i, align_bytes=64) for i in range(3)]
+        planes = [const.tile([P, WIDTH], U8, name="plane%d" % i, align_bytes=64) for i in range(4)]
         rows = const.tile([P, NT], BF16, name="rows")
         ident_b = const.tile([P, P], BF16, name="ident_b")
         ident_f = const.tile([P, P], F32, name="ident_f")
@@ -48,8 +48,8 @@ def tile_input_timestep_w_kernel(tc, t, W1_words, W1_scales, b1, W2_words, W2_sc
         hphi = const.tile([P, 4 * GROUPS], F32, name="hphi")
         cfac = const.tile([P, 4 * GROUPS], F32, name="cfac")
         warm = const.tile([P, 1], F32, name="warm")
-        u = const.tile([P, P], F32, name="u")
-        t2 = const.tile([P, P], F32, name="t2")
+        m2hphi = const.tile([P, 4 * GROUPS], F32, name="m2hphi")
+        cfac2 = const.tile([P, 4 * GROUPS], F32, name="cfac2")
         b1s = const.tile([P, GROUPS, 4, P], BF16, name="b1s")
         b2b = const.tile([P, WIDTH], BF16, name="b2b")
         embq = const.tile([P, GROUPS, P], U32, name="embq", align_bytes=64)
@@ -64,6 +64,7 @@ def tile_input_timestep_w_kernel(tc, t, W1_words, W1_scales, b1, W2_words, W2_sc
         nc.vector.memset(rows[:], 0.0)
         nc.vector.memset(planes[1][:].bitcast(I32), 0)
         nc.vector.memset(planes[2][:].bitcast(I32), 0)
+        nc.vector.memset(planes[3][:].bitcast(I32), 0)
 
         nc.scalar.dma_start(out=rows[12:13, 0:P], in_=t.rearrange("(o n) -> o n", o=1))
         nc.scalar.dma_start(out=rows[0:6, :], in_=b1.rearrange("(c n) -> c n", c=6))
@@ -75,12 +76,6 @@ def tile_input_timestep_w_kernel(tc, t, W1_words, W1_scales, b1, W2_words, W2_sc
         for q in range(4):
             nc.sync.dma_start(out=planes[1][32 * q:32 * q + 8, :].bitcast(I32),
                               in_=W1_scales[4:6, 4 * q:4 * q + 4, :].bitcast(I32))
-        for q in range(4):
-            nc.sync.dma_start(out=planes[1][32 * q + 8:32 * q + 16, :].bitcast(I32),
-                              in_=W2_scales[0:2, 4 * q:4 * q + 4, :].bitcast(I32))
-        for q in range(4):
-            nc.sync.dma_start(out=planes[2][32 * q:32 * q + 16, :].bitcast(I32),
-                              in_=W2_scales[2:6, 4 * q:4 * q + 4, :].bitcast(I32))
         for g in range(GROUPS):
             nc.sync.dma_start(out=w1[g][:].bitcast(I32),
                               in_=W1_words[g].rearrange("p n t -> p (n t)").bitcast(I32))
@@ -94,6 +89,14 @@ def tile_input_timestep_w_kernel(tc, t, W1_words, W1_scales, b1, W2_words, W2_sc
         make_identity(nc, ident_b[:])
         nc.gpsimd.iota(idx[:], pattern=[[NT, GROUPS], [1, 4]], base=0, channel_multiplier=4)
         make_identity(nc, ident_f[:])
+        for r in range(4):
+            for q in (0, 2, 1, 3):
+                nc.gpsimd.dma_start(out=planes[2][32 * q + r:32 * q + 16:4, :].bitcast(F32),
+                                    in_=W2_scales[0:4, 4 * q + r, :].bitcast(F32))
+        for a in range(2):
+            for r in range(4):
+                nc.gpsimd.dma_start(out=planes[3][4 * a + r:P:32, :].bitcast(F32),
+                                    in_=W2_scales[4 + a, r:16:4, :].bitcast(F32))
 
         def spread_row(r):
             ps = auxp.tile([P, NT], F32, name="aux")
@@ -102,11 +105,13 @@ def tile_input_timestep_w_kernel(tc, t, W1_words, W1_scales, b1, W2_words, W2_sc
 
         nc.vector.tensor_copy(out=idxf[:], in_=idx[:])
         nc.vector.tensor_scalar_mul(out=hphi[:], in0=idxf[:], scalar1=math.pi / (2 * WIDTH))
+        nc.vector.tensor_scalar_mul(out=m2hphi[:], in0=idxf[:], scalar1=-math.pi / WIDTH)
         nc.scalar.activation(out=cfac[:], in_=hphi[:], func=ACT.Sin, bias=math.pi / 4, scale=1.0)
+        nc.vector.tensor_scalar_mul(out=cfac2[:], in0=cfac[:], scalar1=2.0)
 
-        tb = spread_row(12)
-        nc.vector.tensor_scalar(out=u[:], in0=tb[:, 0:P], scalar1=-2.0, scalar2=1.0, op0=ALU.mult, op1=ALU.add)
-        nc.vector.tensor_scalar_mul(out=t2[:], in0=tb[:, 0:P], scalar1=2.0)
+        tb = accp.tile([P, NT], F32, name="acc5")
+        nc.tensor.matmul(tb[:], lhsT=ident_b[:, 12:13].to_broadcast([P, P]), rhs=rows[:], start=True, stop=True)
+        tbc = tb[:, 0:P].unsqueeze(2).to_broadcast([P, P, 4])
 
         xs = {}
         cts = {}
@@ -115,12 +120,13 @@ def tile_input_timestep_w_kernel(tc, t, W1_words, W1_scales, b1, W2_words, W2_sc
             if step < GROUPS:
                 g = step
                 x = work.tile([P, P, 4], F32, name="x")
-                nc.vector.tensor_tensor(out=x[:], in0=hphi[:, 4 * g:4 * g + 4].unsqueeze(1).to_broadcast([P, P, 4]),
-                                        in1=u[:].unsqueeze(2).to_broadcast([P, P, 4]), op=ALU.mult)
+                nc.vector.scalar_tensor_tensor(out=x[:], in0=tbc, scalar=0.5,
+                                               in1=m2hphi[:, 4 * g:4 * g + 4].unsqueeze(1).to_broadcast([P, P, 4]),
+                                               op0=ALU.subtract, op1=ALU.mult)
                 nc.scalar.activation(out=x[:], in_=x[:], func=ACT.Sin, bias=math.pi / 4, scale=1.0)
                 ct = work.tile([P, P, 4], F32, name="ct")
-                nc.vector.tensor_tensor(out=ct[:], in0=cfac[:, 4 * g:4 * g + 4].unsqueeze(1).to_broadcast([P, P, 4]),
-                                        in1=t2[:].unsqueeze(2).to_broadcast([P, P, 4]), op=ALU.mult)
+                nc.vector.tensor_tensor(out=ct[:], in0=tbc,
+                                        in1=cfac2[:, 4 * g:4 * g + 4].unsqueeze(1).to_broadcast([P, P, 4]), op=ALU.mult)
                 xs[g] = x
                 cts[g] = ct
                 ps = spread_row(g)

@@ -70,15 +70,22 @@ def tile_input_timestep_w_kernel(tc, t, W1_words, W1_scales, b1, W2_words, W2_sc
         nc.scalar.dma_start(out=rows[0:6, :], in_=b1.rearrange("(c n) -> c n", c=6))
         nc.scalar.dma_start(out=rows[6:12, :], in_=b2.rearrange("(c n) -> c n", c=6))
 
+        def load_w1(g):
+            nc.sync.dma_start(out=w1[g][:].bitcast(I32),
+                              in_=W1_words[g].rearrange("p n t -> p (n t)").bitcast(I32))
+
+        load_w1(0)
+        load_w1(1)
         for q in range(4):
             nc.sync.dma_start(out=planes[0][32 * q:32 * q + 16, :].bitcast(I32),
                               in_=W1_scales[0:4, 4 * q:4 * q + 4, :].bitcast(I32))
+        load_w1(2)
+        load_w1(3)
         for q in range(4):
             nc.sync.dma_start(out=planes[1][32 * q:32 * q + 8, :].bitcast(I32),
                               in_=W1_scales[4:6, 4 * q:4 * q + 4, :].bitcast(I32))
-        for g in range(GROUPS):
-            nc.sync.dma_start(out=w1[g][:].bitcast(I32),
-                              in_=W1_words[g].rearrange("p n t -> p (n t)").bitcast(I32))
+        load_w1(4)
+        load_w1(5)
         for g in range(GROUPS - 1):
             nc.sync.dma_start(out=w2[g][:].bitcast(I32),
                               in_=W2_words[g].rearrange("p n t -> p (n t)").bitcast(I32))

@@ -37,7 +37,7 @@ def tile_input_timestep_w_kernel(tc, t, W1_words, W1_scales, b1, W2_words, W2_sc
         wpool = ctx.enter_context(tc.tile_pool(name="weights", bufs=1))
         work = ctx.enter_context(tc.tile_pool(name="work", bufs=2))
         accp = ctx.enter_context(tc.psum_pool(name="acc", bufs=1))
-        auxp = ctx.enter_context(tc.psum_pool(name="aux", bufs=2))
+        auxp = ctx.enter_context(tc.psum_pool(name="aux", bufs=1))
 
         planes = [const.tile([P, WIDTH], U8, name="plane%d" % i, align_bytes=64) for i in range(4)]
         rows = const.tile([P, NT], BF16, name="rows")
@@ -60,8 +60,8 @@ def tile_input_timestep_w_kernel(tc, t, W1_words, W1_scales, b1, W2_words, W2_sc
         w2 = [wpool.tile([P, WIDTH], U32, name="w2_%d" % g, align_bytes=64) for g in range(GROUPS - 1)]
         w2last = [wpool.tile([P, NT], U32, name="w2l_%d" % c, align_bytes=64) for c in range(BANKS)]
 
-        nc.vector.memset(planes[0][:].bitcast(I32), 0)
         nc.vector.memset(rows[:], 0.0)
+        nc.vector.memset(planes[0][:].bitcast(I32), 0)
         nc.vector.memset(planes[1][:].bitcast(I32), 0)
         nc.vector.memset(planes[2][:].bitcast(I32), 0)
         nc.vector.memset(planes[3][:].bitcast(I32), 0)
@@ -70,22 +70,12 @@ def tile_input_timestep_w_kernel(tc, t, W1_words, W1_scales, b1, W2_words, W2_sc
         nc.scalar.dma_start(out=rows[0:6, :], in_=b1.rearrange("(c n) -> c n", c=6))
         nc.scalar.dma_start(out=rows[6:12, :], in_=b2.rearrange("(c n) -> c n", c=6))
 
-        def load_w1(g):
-            nc.sync.dma_start(out=w1[g][:].bitcast(I32),
-                              in_=W1_words[g].rearrange("p n t -> p (n t)").bitcast(I32))
-
-        load_w1(0)
-        load_w1(1)
         for q in range(4):
             nc.sync.dma_start(out=planes[0][32 * q:32 * q + 16, :].bitcast(I32),
                               in_=W1_scales[0:4, 4 * q:4 * q + 4, :].bitcast(I32))
-        load_w1(2)
-        load_w1(3)
-        for q in range(4):
-            nc.sync.dma_start(out=planes[1][32 * q:32 * q + 8, :].bitcast(I32),
-                              in_=W1_scales[4:6, 4 * q:4 * q + 4, :].bitcast(I32))
-        load_w1(4)
-        load_w1(5)
+        for g in range(GROUPS):
+            nc.sync.dma_start(out=w1[g][:].bitcast(I32),
+                              in_=W1_words[g].rearrange("p n t -> p (n t)").bitcast(I32))
         for g in range(GROUPS - 1):
             nc.sync.dma_start(out=w2[g][:].bitcast(I32),
                               in_=W2_words[g].rearrange("p n t -> p (n t)").bitcast(I32))
@@ -96,6 +86,10 @@ def tile_input_timestep_w_kernel(tc, t, W1_words, W1_scales, b1, W2_words, W2_sc
         make_identity(nc, ident_b[:])
         nc.gpsimd.iota(idx[:], pattern=[[NT, GROUPS], [1, 4]], base=0, channel_multiplier=4)
         make_identity(nc, ident_f[:])
+        for a in range(2):
+            for r in range(4):
+                nc.gpsimd.dma_start(out=planes[1][4 * a + r:P:32, :].bitcast(F32),
+                                    in_=W1_scales[4 + a, r:16:4, :].bitcast(F32))
         for r in range(4):
             for q in (0, 2, 1, 3):
                 nc.gpsimd.dma_start(out=planes[2][32 * q + r:32 * q + 16:4, :].bitcast(F32),
@@ -105,8 +99,8 @@ def tile_input_timestep_w_kernel(tc, t, W1_words, W1_scales, b1, W2_words, W2_sc
                 nc.gpsimd.dma_start(out=planes[3][4 * a + r:P:32, :].bitcast(F32),
                                     in_=W2_scales[4 + a, r:16:4, :].bitcast(F32))
 
-        def spread_row(r):
-            ps = auxp.tile([P, NT], F32, name="aux")
+        def spread_row(r, bank):
+            ps = auxp.tile([P, NT], F32, name="aux%d" % bank)
             nc.tensor.matmul(ps[:], lhsT=ident_b[:, r:r + 1].to_broadcast([P, P]), rhs=rows[:], start=True, stop=True)
             return ps
 
@@ -116,8 +110,7 @@ def tile_input_timestep_w_kernel(tc, t, W1_words, W1_scales, b1, W2_words, W2_sc
         nc.scalar.activation(out=cfac[:], in_=hphi[:], func=ACT.Sin, bias=math.pi / 4, scale=1.0)
         nc.vector.tensor_scalar_mul(out=cfac2[:], in0=cfac[:], scalar1=2.0)
 
-        tb = accp.tile([P, NT], F32, name="acc5")
-        nc.tensor.matmul(tb[:], lhsT=ident_b[:, 12:13].to_broadcast([P, P]), rhs=rows[:], start=True, stop=True)
+        tb = spread_row(12, 0)
         tbc = tb[:, 0:P].unsqueeze(2).to_broadcast([P, P, 4])
 
         xs = {}
@@ -136,8 +129,6 @@ def tile_input_timestep_w_kernel(tc, t, W1_words, W1_scales, b1, W2_words, W2_sc
                                         in1=cfac2[:, 4 * g:4 * g + 4].unsqueeze(1).to_broadcast([P, P, 4]), op=ALU.mult)
                 xs[g] = x
                 cts[g] = ct
-                ps = spread_row(g)
-                nc.scalar.copy(out=b1s[:, g], in_=ps[:].rearrange("p (q t) -> p t q", t=4))
             if 1 <= step <= GROUPS:
                 g = step - 1
                 eg = work.tile([P, P, 4], BF16, name="eg", align_bytes=64)
@@ -157,8 +148,10 @@ def tile_input_timestep_w_kernel(tc, t, W1_words, W1_scales, b1, W2_words, W2_sc
                 nc.tensor.matmul_mx(out=acc1[c][:], lhsT=embq[:, g, :].bitcast(FP8X4), lhsT_scale=embs[:, g, :],
                                     rhs=w1[g][:, cols].bitcast(FP8X4), rhs_scale=planes[pi][k:P, cols],
                                     start=(g == 0), stop=(g == GROUPS - 1))
-            ps = spread_row(6 + g)
-            nc.scalar.copy(out=b2b[:, g * NT:(g + 1) * NT], in_=ps[:])
+            if g in (2, 3, 4):
+                for c in (2 * (g - 2), 2 * (g - 2) + 1):
+                    ps = spread_row(c, c % 2)
+                    nc.scalar.copy(out=b1s[:, c], in_=ps[:].rearrange("p (q t) -> p t q", t=4))
 
         hgs = {}
         for step in range(GROUPS + 2):
@@ -166,7 +159,7 @@ def tile_input_timestep_w_kernel(tc, t, W1_words, W1_scales, b1, W2_words, W2_sc
                 c = step
                 z = work.tile([P, 4, P], F32, name="z", bufs=3)
                 nc.vector.tensor_tensor(out=z[:], in0=acc1[c][:].rearrange("p (q t) -> p t q", t=4), in1=b1s[:, c], op=ALU.add)
-                xt = auxp.tile([P, NT], F32, name="aux")
+                xt = auxp.tile([P, NT], F32, name="aux%d" % (c % 2))
                 for j in range(4):
                     nc.tensor.transpose(xt[:, j * P:(j + 1) * P], z[:, j, :], ident_f[:])
                 hg = work.tile([P, P, 4], BF16, name="hg", bufs=3, align_bytes=64)
@@ -185,6 +178,9 @@ def tile_input_timestep_w_kernel(tc, t, W1_words, W1_scales, b1, W2_words, W2_sc
                 nc.tensor.matmul_mx(out=acc2[c][:], lhsT=hq[:, g, :].bitcast(FP8X4), lhsT_scale=hs[:, g, :],
                                     rhs=w2[g][:, cols].bitcast(FP8X4), rhs_scale=planes[pi][k:P, cols],
                                     start=(g == 0), stop=False)
+            for c in ((g,) if g < GROUPS - 2 else (g, g + 1)):
+                ps = spread_row(6 + c, c % 2)
+                nc.scalar.copy(out=b2b[:, c * NT:(c + 1) * NT], in_=ps[:])
         g = GROUPS - 1
         pi, k = w2_plane(g)
         for c in range(BANKS):

@@ -15,6 +15,7 @@ ACT = mybir.ActivationFunctionType
 
 P = 128
 WIDTH = 3072
+HALF = 1536
 GROUPS = 6
 NT = 512
 BANKS = 6
@@ -46,22 +47,23 @@ def tile_input_timestep_w_kernel(tc, t, W1_words, W1_scales, b1, W2_words, W2_sc
         idx = const.tile([P, 4 * GROUPS], I32, name="idx")
         idxf = const.tile([P, 4 * GROUPS], F32, name="idxf")
         hphi = const.tile([P, 4 * GROUPS], F32, name="hphi")
-        cfac = const.tile([P, 4 * GROUPS], F32, name="cfac")
-        warm = const.tile([P, 1], F32, name="warm")
         m2hphi = const.tile([P, 4 * GROUPS], F32, name="m2hphi")
+        cfac = const.tile([P, 4 * GROUPS], F32, name="cfac")
         cfac2 = const.tile([P, 4 * GROUPS], F32, name="cfac2")
+        warm = const.tile([P, 1], F32, name="warm")
         b1s = const.tile([P, GROUPS, 4, P], BF16, name="b1s")
         b2b = const.tile([P, WIDTH], BF16, name="b2b")
         embq = const.tile([P, GROUPS, P], U32, name="embq", align_bytes=64)
         embs = const.tile([P, GROUPS, P], U8, name="embs", align_bytes=64)
         hq = const.tile([P, GROUPS, P], U32, name="hq", align_bytes=64)
         hs = const.tile([P, GROUPS, P], U8, name="hs", align_bytes=64)
-        w1 = [wpool.tile([P, WIDTH], U32, name="w1_%d" % g, align_bytes=64) for g in range(GROUPS)]
+        w1 = [[wpool.tile([P, HALF], U32, name="w1_%d_%d" % (s, g), align_bytes=64) for g in range(GROUPS)]
+              for s in range(2)]
         w2 = [wpool.tile([P, WIDTH], U32, name="w2_%d" % g, align_bytes=64) for g in range(GROUPS - 1)]
         w2last = [wpool.tile([P, NT], U32, name="w2l_%d" % c, align_bytes=64) for c in range(BANKS)]
 
-        nc.vector.memset(rows[:], 0.0)
         nc.vector.memset(planes[0][:].bitcast(I32), 0)
+        nc.vector.memset(rows[:], 0.0)
         nc.vector.memset(planes[1][:].bitcast(I32), 0)
         nc.vector.memset(planes[2][:].bitcast(I32), 0)
         nc.vector.memset(planes[3][:].bitcast(I32), 0)
@@ -73,9 +75,13 @@ def tile_input_timestep_w_kernel(tc, t, W1_words, W1_scales, b1, W2_words, W2_sc
         for q in range(4):
             nc.sync.dma_start(out=planes[0][32 * q:32 * q + 16, :].bitcast(I32),
                               in_=W1_scales[0:4, 4 * q:4 * q + 4, :].bitcast(I32))
-        for g in range(GROUPS):
-            nc.sync.dma_start(out=w1[g][:].bitcast(I32),
-                              in_=W1_words[g].rearrange("p n t -> p (n t)").bitcast(I32))
+        for q in range(4):
+            nc.sync.dma_start(out=planes[1][32 * q:32 * q + 8, :].bitcast(I32),
+                              in_=W1_scales[4:6, 4 * q:4 * q + 4, :].bitcast(I32))
+        for s in range(2):
+            for g in range(GROUPS):
+                nc.sync.dma_start(out=w1[s][g][:].bitcast(I32),
+                                  in_=W1_words[g].rearrange("p n t -> p (n t)")[:, 4 * HALF * s:4 * HALF * (s + 1)].bitcast(I32))
         for g in range(GROUPS - 1):
             nc.sync.dma_start(out=w2[g][:].bitcast(I32),
                               in_=W2_words[g].rearrange("p n t -> p (n t)").bitcast(I32))
@@ -86,10 +92,6 @@ def tile_input_timestep_w_kernel(tc, t, W1_words, W1_scales, b1, W2_words, W2_sc
         make_identity(nc, ident_b[:])
         nc.gpsimd.iota(idx[:], pattern=[[NT, GROUPS], [1, 4]], base=0, channel_multiplier=4)
         make_identity(nc, ident_f[:])
-        for a in range(2):
-            for r in range(4):
-                nc.gpsimd.dma_start(out=planes[1][4 * a + r:P:32, :].bitcast(F32),
-                                    in_=W1_scales[4 + a, r:16:4, :].bitcast(F32))
         for r in range(4):
             for q in (0, 2, 1, 3):
                 nc.gpsimd.dma_start(out=planes[2][32 * q + r:32 * q + 16:4, :].bitcast(F32),
@@ -99,10 +101,41 @@ def tile_input_timestep_w_kernel(tc, t, W1_words, W1_scales, b1, W2_words, W2_sc
                 nc.gpsimd.dma_start(out=planes[3][4 * a + r:P:32, :].bitcast(F32),
                                     in_=W2_scales[4 + a, r:16:4, :].bitcast(F32))
 
-        def spread_row(r, bank):
-            ps = auxp.tile([P, NT], F32, name="aux%d" % bank)
+        def spread_row(ps, r):
             nc.tensor.matmul(ps[:], lhsT=ident_b[:, r:r + 1].to_broadcast([P, P]), rhs=rows[:], start=True, stop=True)
-            return ps
+
+        def spread_bias(k):
+            ps = auxp.tile([P, NT], F32, name="aux%d" % (k % 2))
+            spread_row(ps, k)
+            if k < GROUPS:
+                nc.scalar.copy(out=b1s[:, k], in_=ps[:].rearrange("p (q t) -> p t q", t=4))
+            else:
+                nc.scalar.copy(out=b2b[:, (k - GROUPS) * NT:(k - GROUPS + 1) * NT], in_=ps[:])
+
+        acc1 = {}
+
+        def layer1_passes(g, banks):
+            pi, k = w1_plane(g)
+            for c in banks:
+                nc.tensor.matmul_mx(out=acc1[c][:], lhsT=embq[:, g, :].bitcast(FP8X4), lhsT_scale=embs[:, g, :],
+                                    rhs=w1[c // 3][g][:, (c % 3) * NT:(c % 3 + 1) * NT].bitcast(FP8X4),
+                                    rhs_scale=planes[pi][k:P, c * NT:(c + 1) * NT],
+                                    start=(g == 0), stop=(g == GROUPS - 1))
+
+        def h_banks(banks):
+            hgs = {}
+            for c in banks:
+                z = work.tile([P, 4, P], F32, name="z", bufs=3)
+                nc.vector.tensor_tensor(out=z[:], in0=acc1[c][:].rearrange("p (q t) -> p t q", t=4), in1=b1s[:, c], op=ALU.add)
+                xt = auxp.tile([P, NT], F32, name="aux%d" % (c % 2))
+                for j in range(4):
+                    nc.tensor.transpose(xt[:, j * P:(j + 1) * P], z[:, j, :], ident_f[:])
+                hg = work.tile([P, P, 4], BF16, name="hg", bufs=3, align_bytes=64)
+                nc.scalar.activation(out=hg[:], in_=xt[:].rearrange("p (t r) -> p r t", t=4), func=ACT.Silu)
+                hgs[c] = hg
+            for c in banks:
+                nc.vector.quantize_mx(out=hq[:, c, :].bitcast(FP8X4), scales=hs[:, c, :],
+                                      in_=hgs[c][:].rearrange("p b j -> p (b j)"))
 
         nc.vector.tensor_copy(out=idxf[:], in_=idx[:])
         nc.vector.tensor_scalar_mul(out=hphi[:], in0=idxf[:], scalar1=math.pi / (2 * WIDTH))
@@ -110,8 +143,11 @@ def tile_input_timestep_w_kernel(tc, t, W1_words, W1_scales, b1, W2_words, W2_sc
         nc.scalar.activation(out=cfac[:], in_=hphi[:], func=ACT.Sin, bias=math.pi / 4, scale=1.0)
         nc.vector.tensor_scalar_mul(out=cfac2[:], in0=cfac[:], scalar1=2.0)
 
-        tb = spread_row(12, 0)
+        tb = accp.tile([P, NT], F32, name="acc5")
+        spread_row(tb, 12)
         tbc = tb[:, 0:P].unsqueeze(2).to_broadcast([P, P, 4])
+        for c in range(3):
+            acc1[c] = accp.tile([P, NT], F32, name="acc%d" % c)
 
         xs = {}
         cts = {}
@@ -124,6 +160,8 @@ def tile_input_timestep_w_kernel(tc, t, W1_words, W1_scales, b1, W2_words, W2_sc
                                                in1=m2hphi[:, 4 * g:4 * g + 4].unsqueeze(1).to_broadcast([P, P, 4]),
                                                op0=ALU.subtract, op1=ALU.mult)
                 nc.scalar.activation(out=x[:], in_=x[:], func=ACT.Sin, bias=math.pi / 4, scale=1.0)
+                if g == GROUPS - 1:
+                    nc.scalar.activation(out=warm[:], in_=hphi[:, 0:1], func=ACT.Silu)
                 ct = work.tile([P, P, 4], F32, name="ct")
                 nc.vector.tensor_tensor(out=ct[:], in0=tbc,
                                         in1=cfac2[:, 4 * g:4 * g + 4].unsqueeze(1).to_broadcast([P, P, 4]), op=ALU.mult)
@@ -138,37 +176,18 @@ def tile_input_timestep_w_kernel(tc, t, W1_words, W1_scales, b1, W2_words, W2_sc
                 g = step - 2
                 nc.vector.quantize_mx(out=embq[:, g, :].bitcast(FP8X4), scales=embs[:, g, :],
                                       in_=egs[g][:].rearrange("p b j -> p (b j)"))
-        nc.scalar.activation(out=warm[:], in_=hphi[:, 0:1], func=ACT.Silu)
+                spread_bias(2 * g)
+                spread_bias(2 * g + 1)
+                layer1_passes(g, (0, 1, 2))
 
-        acc1 = [accp.tile([P, NT], F32, name="acc%d" % c) for c in range(BANKS)]
-        for g in range(GROUPS):
-            pi, k = w1_plane(g)
-            for c in range(BANKS):
-                cols = slice(c * NT, (c + 1) * NT)
-                nc.tensor.matmul_mx(out=acc1[c][:], lhsT=embq[:, g, :].bitcast(FP8X4), lhsT_scale=embs[:, g, :],
-                                    rhs=w1[g][:, cols].bitcast(FP8X4), rhs_scale=planes[pi][k:P, cols],
-                                    start=(g == 0), stop=(g == GROUPS - 1))
-            if g in (2, 3, 4):
-                for c in (2 * (g - 2), 2 * (g - 2) + 1):
-                    ps = spread_row(c, c % 2)
-                    nc.scalar.copy(out=b1s[:, c], in_=ps[:].rearrange("p (q t) -> p t q", t=4))
-
-        hgs = {}
-        for step in range(GROUPS + 2):
-            if step < GROUPS:
-                c = step
-                z = work.tile([P, 4, P], F32, name="z", bufs=3)
-                nc.vector.tensor_tensor(out=z[:], in0=acc1[c][:].rearrange("p (q t) -> p t q", t=4), in1=b1s[:, c], op=ALU.add)
-                xt = auxp.tile([P, NT], F32, name="aux%d" % (c % 2))
-                for j in range(4):
-                    nc.tensor.transpose(xt[:, j * P:(j + 1) * P], z[:, j, :], ident_f[:])
-                hg = work.tile([P, P, 4], BF16, name="hg", bufs=3, align_bytes=64)
-                nc.scalar.activation(out=hg[:], in_=xt[:].rearrange("p (t r) -> p r t", t=4), func=ACT.Silu)
-                hgs[c] = hg
-            if step >= 2:
-                c = step - 2
-                nc.vector.quantize_mx(out=hq[:, c, :].bitcast(FP8X4), scales=hs[:, c, :],
-                                      in_=hgs[c][:].rearrange("p b j -> p (b j)"))
+        for c in range(3, BANKS):
+            acc1[c] = accp.tile([P, NT], F32, name="acc%d" % c)
+        layer1_passes(0, (3, 4, 5))
+        layer1_passes(1, (3, 4, 5))
+        h_banks((0, 1, 2))
+        for g in range(2, GROUPS):
+            layer1_passes(g, (3, 4, 5))
+        h_banks((3, 4, 5))
 
         acc2 = [accp.tile([P, NT], F32, name="acc%d" % c) for c in range(BANKS)]
         for g in range(GROUPS - 1):
@@ -178,9 +197,6 @@ def tile_input_timestep_w_kernel(tc, t, W1_words, W1_scales, b1, W2_words, W2_sc
                 nc.tensor.matmul_mx(out=acc2[c][:], lhsT=hq[:, g, :].bitcast(FP8X4), lhsT_scale=hs[:, g, :],
                                     rhs=w2[g][:, cols].bitcast(FP8X4), rhs_scale=planes[pi][k:P, cols],
                                     start=(g == 0), stop=False)
-            for c in ((g,) if g < GROUPS - 2 else (g, g + 1)):
-                ps = spread_row(6 + c, c % 2)
-                nc.scalar.copy(out=b2b[:, c * NT:(c + 1) * NT], in_=ps[:])
         g = GROUPS - 1
         pi, k = w2_plane(g)
         for c in range(BANKS):

@@ -23,11 +23,11 @@ FLOPS = 2 * 2 * 128 * 3072 * 3072
 
 
 def w1_plane(g):
-    return (0, 4 * g) if g < 4 else (1, 4 * (g - 4))
+    return (g // 4, 4 * (g % 4))
 
 
 def w2_plane(g):
-    return (2, 4 * g) if g < 4 else (3, 4 * (g - 4))
+    return ((g + GROUPS) // 4, 4 * ((g + GROUPS) % 4))
 
 
 def tile_input_timestep_w_kernel(tc, t, W1_words, W1_scales, b1, W2_words, W2_scales, b2, out):
@@ -40,7 +40,7 @@ def tile_input_timestep_w_kernel(tc, t, W1_words, W1_scales, b1, W2_words, W2_sc
         accp = ctx.enter_context(tc.psum_pool(name="acc", bufs=1))
         auxp = ctx.enter_context(tc.psum_pool(name="aux", bufs=1))
 
-        planes = [const.tile([P, WIDTH], U8, name="plane%d" % i, align_bytes=64) for i in range(4)]
+        planes = [const.tile([P, WIDTH], U8, name="plane%d" % i, align_bytes=64) for i in range(3)]
         rows = const.tile([P, NT], BF16, name="rows")
         ident_b = const.tile([P, P], BF16, name="ident_b")
         ident_f = const.tile([P, P], F32, name="ident_f")
@@ -66,18 +66,11 @@ def tile_input_timestep_w_kernel(tc, t, W1_words, W1_scales, b1, W2_words, W2_sc
         nc.vector.memset(rows[:], 0.0)
         nc.vector.memset(planes[1][:].bitcast(I32), 0)
         nc.vector.memset(planes[2][:].bitcast(I32), 0)
-        nc.vector.memset(planes[3][:].bitcast(I32), 0)
 
         nc.scalar.dma_start(out=rows[12:13, 0:P], in_=t.rearrange("(o n) -> o n", o=1))
         nc.scalar.dma_start(out=rows[0:6, :], in_=b1.rearrange("(c n) -> c n", c=6))
         nc.scalar.dma_start(out=rows[6:12, :], in_=b2.rearrange("(c n) -> c n", c=6))
 
-        for q in range(4):
-            nc.sync.dma_start(out=planes[0][32 * q:32 * q + 16, :].bitcast(I32),
-                              in_=W1_scales[0:4, 4 * q:4 * q + 4, :].bitcast(I32))
-        for q in range(4):
-            nc.sync.dma_start(out=planes[1][32 * q:32 * q + 8, :].bitcast(I32),
-                              in_=W1_scales[4:6, 4 * q:4 * q + 4, :].bitcast(I32))
         for s in range(2):
             for g in range(GROUPS):
                 nc.sync.dma_start(out=w1[s][g][:].bitcast(I32),
@@ -91,15 +84,17 @@ def tile_input_timestep_w_kernel(tc, t, W1_words, W1_scales, b1, W2_words, W2_sc
 
         make_identity(nc, ident_b[:])
         nc.gpsimd.iota(idx[:], pattern=[[NT, GROUPS], [1, 4]], base=0, channel_multiplier=4)
+
+        def load_planes(tile, k, scales, g, n):
+            for q in range(4):
+                nc.gpsimd.dma_start(out=planes[tile][32 * q + k:32 * q + k + 4 * n, :].bitcast(F32),
+                                    in_=scales[g:g + n, 4 * q:4 * q + 4, :].bitcast(F32))
+
+        load_planes(0, 0, W1_scales, 0, 4)
+        load_planes(1, 0, W1_scales, 4, 2)
         make_identity(nc, ident_f[:])
-        for r in range(4):
-            for q in (0, 2, 1, 3):
-                nc.gpsimd.dma_start(out=planes[2][32 * q + r:32 * q + 16:4, :].bitcast(F32),
-                                    in_=W2_scales[0:4, 4 * q + r, :].bitcast(F32))
-        for a in range(2):
-            for r in range(4):
-                nc.gpsimd.dma_start(out=planes[3][4 * a + r:P:32, :].bitcast(F32),
-                                    in_=W2_scales[4 + a, r:16:4, :].bitcast(F32))
+        load_planes(1, 8, W2_scales, 0, 2)
+        load_planes(2, 0, W2_scales, 2, 4)
 
         def spread_row(ps, r):
             nc.tensor.matmul(ps[:], lhsT=ident_b[:, r:r + 1].to_broadcast([P, P]), rhs=rows[:], start=True, stop=True)

@@ -71,10 +71,19 @@ def tile_input_timestep_w_kernel(tc, t, W1_words, W1_scales, b1, W2_words, W2_sc
         nc.scalar.dma_start(out=rows[0:6, :], in_=b1.rearrange("(c n) -> c n", c=6))
         nc.scalar.dma_start(out=rows[6:12, :], in_=b2.rearrange("(c n) -> c n", c=6))
 
+        def load_planes(queue, dtype, quadrants, tile, k, scales, g, n):
+            for q in quadrants:
+                queue.dma_start(out=planes[tile][32 * q + k:32 * q + k + 4 * n, :].bitcast(dtype),
+                                in_=scales[g:g + n, 4 * q:4 * q + 4, :].bitcast(dtype))
+
+        plane_loads = [(0, 0, W1_scales, 0, 4), (1, 0, W1_scales, 4, 2), (1, 8, W2_scales, 0, 2), (2, 0, W2_scales, 2, 4)]
+
         for s in range(2):
             for g in range(GROUPS):
                 nc.sync.dma_start(out=w1[s][g][:].bitcast(I32),
                                   in_=W1_words[g].rearrange("p n t -> p (n t)")[:, 4 * HALF * s:4 * HALF * (s + 1)].bitcast(I32))
+                if s == 0 and g < 4:
+                    load_planes(nc.sync, I32, (0, 1), *plane_loads[g])
         for g in range(GROUPS - 1):
             nc.sync.dma_start(out=w2[g][:].bitcast(I32),
                               in_=W2_words[g].rearrange("p n t -> p (n t)").bitcast(I32))
@@ -85,16 +94,11 @@ def tile_input_timestep_w_kernel(tc, t, W1_words, W1_scales, b1, W2_words, W2_sc
         make_identity(nc, ident_b[:])
         nc.gpsimd.iota(idx[:], pattern=[[NT, GROUPS], [1, 4]], base=0, channel_multiplier=4)
 
-        def load_planes(tile, k, scales, g, n):
-            for q in range(4):
-                nc.gpsimd.dma_start(out=planes[tile][32 * q + k:32 * q + k + 4 * n, :].bitcast(F32),
-                                    in_=scales[g:g + n, 4 * q:4 * q + 4, :].bitcast(F32))
-
-        load_planes(0, 0, W1_scales, 0, 4)
-        load_planes(1, 0, W1_scales, 4, 2)
+        load_planes(nc.gpsimd, F32, (2, 3), *plane_loads[0])
+        load_planes(nc.gpsimd, F32, (2, 3), *plane_loads[1])
         make_identity(nc, ident_f[:])
-        load_planes(1, 8, W2_scales, 0, 2)
-        load_planes(2, 0, W2_scales, 2, 4)
+        load_planes(nc.gpsimd, F32, (2, 3), *plane_loads[2])
+        load_planes(nc.gpsimd, F32, (2, 3), *plane_loads[3])
 
         def spread_row(ps, r):
             nc.tensor.matmul(ps[:], lhsT=ident_b[:, r:r + 1].to_broadcast([P, P]), rhs=rows[:], start=True, stop=True)

@@ -41,16 +41,18 @@ def tile_input_timestep_w_kernel(tc, t, W1_words, W1_scales, b1, W2_words, W2_sc
         auxp = ctx.enter_context(tc.psum_pool(name="aux", bufs=1))
 
         planes = [const.tile([P, WIDTH], U8, name="plane%d" % i, align_bytes=64) for i in range(3)]
+        trow = const.tile([P, P], BF16, name="trow")
         rows = const.tile([P, NT], BF16, name="rows")
         ident_b = const.tile([P, P], BF16, name="ident_b")
         ident_f = const.tile([P, P], F32, name="ident_f")
         idx = const.tile([P, 4 * GROUPS], I32, name="idx")
         idxf = const.tile([P, 4 * GROUPS], F32, name="idxf")
-        hphi = const.tile([P, 4 * GROUPS], F32, name="hphi")
-        m2hphi = const.tile([P, 4 * GROUPS], F32, name="m2hphi")
+        slope = const.tile([P, 4 * GROUPS], F32, name="slope")
+        shift = const.tile([P, 4 * GROUPS], F32, name="shift")
         cfac = const.tile([P, 4 * GROUPS], F32, name="cfac")
         cfac2 = const.tile([P, 4 * GROUPS], F32, name="cfac2")
         warm = const.tile([P, 1], F32, name="warm")
+        tbs = const.tile([P, P], F32, name="tbs")
         b1s = const.tile([P, GROUPS, 4, P], BF16, name="b1s")
         b2b = const.tile([P, WIDTH], BF16, name="b2b")
         embq = const.tile([P, GROUPS, P], U32, name="embq", align_bytes=64)
@@ -62,14 +64,11 @@ def tile_input_timestep_w_kernel(tc, t, W1_words, W1_scales, b1, W2_words, W2_sc
         w2 = [wpool.tile([P, WIDTH], U32, name="w2_%d" % g, align_bytes=64) for g in range(GROUPS - 1)]
         w2last = [wpool.tile([P, NT], U32, name="w2l_%d" % c, align_bytes=64) for c in range(BANKS)]
 
+        nc.vector.memset(trow[:], 0.0)
         nc.vector.memset(planes[0][:].bitcast(I32), 0)
         nc.vector.memset(rows[:], 0.0)
         nc.vector.memset(planes[1][:].bitcast(I32), 0)
         nc.vector.memset(planes[2][:].bitcast(I32), 0)
-
-        nc.scalar.dma_start(out=rows[12:13, 0:P], in_=t.rearrange("(o n) -> o n", o=1))
-        nc.scalar.dma_start(out=rows[0:6, :], in_=b1.rearrange("(c n) -> c n", c=6))
-        nc.scalar.dma_start(out=rows[6:12, :], in_=b2.rearrange("(c n) -> c n", c=6))
 
         def load_planes(queue, dtype, quadrants, tile, k, scales, g, n):
             for q in quadrants:
@@ -78,38 +77,53 @@ def tile_input_timestep_w_kernel(tc, t, W1_words, W1_scales, b1, W2_words, W2_sc
 
         plane_loads = [(0, 0, W1_scales, 0, 4), (1, 0, W1_scales, 4, 2), (1, 8, W2_scales, 0, 2), (2, 0, W2_scales, 2, 4)]
 
+        def load_words(tile, words, c, w):
+            nc.sync.dma_start(out=tile[:].bitcast(I32),
+                              in_=words.rearrange("p n t -> p (n t)")[:, 4 * c:4 * (c + w)].bitcast(I32))
+
+        nc.scalar.dma_start(out=trow[0:1, :], in_=t.rearrange("(o n) -> o n", o=1))
+        nc.scalar.dma_start(out=rows[0:6, :], in_=b1.rearrange("(c n) -> c n", c=6))
+        nc.scalar.dma_start(out=rows[6:12, :], in_=b2.rearrange("(c n) -> c n", c=6))
         for s in range(2):
             for g in range(GROUPS):
-                nc.sync.dma_start(out=w1[s][g][:].bitcast(I32),
-                                  in_=W1_words[g].rearrange("p n t -> p (n t)")[:, 4 * HALF * s:4 * HALF * (s + 1)].bitcast(I32))
+                load_words(w1[s][g], W1_words[g], s * HALF, HALF)
                 if s == 0 and g < 4:
                     load_planes(nc.sync, I32, (0, 1), *plane_loads[g])
         for g in range(GROUPS - 1):
-            nc.sync.dma_start(out=w2[g][:].bitcast(I32),
-                              in_=W2_words[g].rearrange("p n t -> p (n t)").bitcast(I32))
+            load_words(w2[g], W2_words[g], 0, WIDTH)
         for c in range(BANKS):
-            nc.sync.dma_start(out=w2last[c][:].bitcast(I32),
-                              in_=W2_words[GROUPS - 1].rearrange("p n t -> p (n t)")[:, 4 * NT * c:4 * NT * (c + 1)].bitcast(I32))
+            load_words(w2last[c], W2_words[GROUPS - 1], c * NT, NT)
 
         make_identity(nc, ident_b[:])
         nc.gpsimd.iota(idx[:], pattern=[[NT, GROUPS], [1, 4]], base=0, channel_multiplier=4)
-
         load_planes(nc.gpsimd, F32, (2, 3), *plane_loads[0])
         load_planes(nc.gpsimd, F32, (2, 3), *plane_loads[1])
         make_identity(nc, ident_f[:])
         load_planes(nc.gpsimd, F32, (2, 3), *plane_loads[2])
         load_planes(nc.gpsimd, F32, (2, 3), *plane_loads[3])
 
-        def spread_row(ps, r):
-            nc.tensor.matmul(ps[:], lhsT=ident_b[:, r:r + 1].to_broadcast([P, P]), rhs=rows[:], start=True, stop=True)
+        nc.vector.tensor_copy(out=idxf[:], in_=idx[:])
+        nc.vector.tensor_scalar_mul(out=slope[:], in0=idxf[:], scalar1=-math.pi / WIDTH)
+        nc.vector.tensor_scalar(out=shift[:], in0=idxf[:], scalar1=math.pi / (2 * WIDTH), scalar2=math.pi / 4,
+                                op0=ALU.mult, op1=ALU.add)
+        nc.scalar.activation(out=cfac[:], in_=shift[:], func=ACT.Sin)
+        nc.vector.tensor_scalar_mul(out=cfac2[:], in0=cfac[:], scalar1=2.0)
 
-        def spread_bias(k):
-            ps = auxp.tile([P, NT], F32, name="aux%d" % (k % 2))
-            spread_row(ps, k)
+        tb = auxp.tile([P, NT], F32, name="aux1")
+        nc.tensor.matmul(tb[:, 0:P], lhsT=ident_b[:, 0:1].to_broadcast([P, P]), rhs=trow[:], start=True, stop=True)
+        nc.scalar.copy(out=tbs[:], in_=tb[:, 0:P])
+
+        spread = {}
+
+        def spread_bias(k, pool, bank):
+            spread[k] = pool.tile([P, NT], F32, name=bank)
+            nc.tensor.matmul(spread[k][:], lhsT=ident_b[:, k:k + 1].to_broadcast([P, P]), rhs=rows[:], start=True, stop=True)
+
+        def keep_bias(k):
             if k < GROUPS:
-                nc.scalar.copy(out=b1s[:, k], in_=ps[:].rearrange("p (q t) -> p t q", t=4))
+                nc.scalar.copy(out=b1s[:, k], in_=spread[k][:].rearrange("p (q t) -> p t q", t=4))
             else:
-                nc.scalar.copy(out=b2b[:, (k - GROUPS) * NT:(k - GROUPS + 1) * NT], in_=ps[:])
+                nc.scalar.copy(out=b2b[:, (k - GROUPS) * NT:(k - GROUPS + 1) * NT], in_=spread[k][:])
 
         acc1 = {}
 
@@ -121,30 +135,8 @@ def tile_input_timestep_w_kernel(tc, t, W1_words, W1_scales, b1, W2_words, W2_sc
                                     rhs_scale=planes[pi][k:P, c * NT:(c + 1) * NT],
                                     start=(g == 0), stop=(g == GROUPS - 1))
 
-        def h_banks(banks):
-            hgs = {}
-            for c in banks:
-                z = work.tile([P, 4, P], F32, name="z", bufs=3)
-                nc.vector.tensor_tensor(out=z[:], in0=acc1[c][:].rearrange("p (q t) -> p t q", t=4), in1=b1s[:, c], op=ALU.add)
-                xt = auxp.tile([P, NT], F32, name="aux%d" % (c % 2))
-                for j in range(4):
-                    nc.tensor.transpose(xt[:, j * P:(j + 1) * P], z[:, j, :], ident_f[:])
-                hg = work.tile([P, P, 4], BF16, name="hg", bufs=3, align_bytes=64)
-                nc.scalar.activation(out=hg[:], in_=xt[:].rearrange("p (t r) -> p r t", t=4), func=ACT.Silu)
-                hgs[c] = hg
-            for c in banks:
-                nc.vector.quantize_mx(out=hq[:, c, :].bitcast(FP8X4), scales=hs[:, c, :],
-                                      in_=hgs[c][:].rearrange("p b j -> p (b j)"))
-
-        nc.vector.tensor_copy(out=idxf[:], in_=idx[:])
-        nc.vector.tensor_scalar_mul(out=hphi[:], in0=idxf[:], scalar1=math.pi / (2 * WIDTH))
-        nc.vector.tensor_scalar_mul(out=m2hphi[:], in0=idxf[:], scalar1=-math.pi / WIDTH)
-        nc.scalar.activation(out=cfac[:], in_=hphi[:], func=ACT.Sin, bias=math.pi / 4, scale=1.0)
-        nc.vector.tensor_scalar_mul(out=cfac2[:], in0=cfac[:], scalar1=2.0)
-
-        tb = accp.tile([P, NT], F32, name="acc5")
-        spread_row(tb, 12)
-        tbc = tb[:, 0:P].unsqueeze(2).to_broadcast([P, P, 4])
+        for k, (pool, bank) in enumerate([(accp, "acc3"), (accp, "acc4"), (accp, "acc5"), (auxp, "aux0"), (auxp, "aux1")]):
+            spread_bias(k, pool, bank)
         for c in range(3):
             acc1[c] = accp.tile([P, NT], F32, name="acc%d" % c)
 
@@ -154,55 +146,79 @@ def tile_input_timestep_w_kernel(tc, t, W1_words, W1_scales, b1, W2_words, W2_sc
         for step in range(GROUPS + 2):
             if step < GROUPS:
                 g = step
-                x = work.tile([P, P, 4], F32, name="x")
-                nc.vector.scalar_tensor_tensor(out=x[:], in0=tbc, scalar=0.5,
-                                               in1=m2hphi[:, 4 * g:4 * g + 4].unsqueeze(1).to_broadcast([P, P, 4]),
-                                               op0=ALU.subtract, op1=ALU.mult)
-                nc.scalar.activation(out=x[:], in_=x[:], func=ACT.Sin, bias=math.pi / 4, scale=1.0)
-                if g == GROUPS - 1:
-                    nc.scalar.activation(out=warm[:], in_=hphi[:, 0:1], func=ACT.Silu)
+                x = work.tile([P, 4, P], F32, name="x", bufs=3)
+                for j in range(4):
+                    m = 4 * g + j
+                    nc.scalar.activation(out=x[:, j, :], in_=tbs[:], func=ACT.Sin,
+                                         bias=shift[:, m:m + 1], scale=slope[:, m:m + 1])
+                if g >= 1:
+                    keep_bias(g - 1)
                 ct = work.tile([P, P, 4], F32, name="ct")
-                nc.vector.tensor_tensor(out=ct[:], in0=tbc,
+                nc.vector.tensor_tensor(out=ct[:], in0=tbs[:].unsqueeze(2).to_broadcast([P, P, 4]),
                                         in1=cfac2[:, 4 * g:4 * g + 4].unsqueeze(1).to_broadcast([P, P, 4]), op=ALU.mult)
                 xs[g] = x
                 cts[g] = ct
+            if step == GROUPS:
+                nc.scalar.activation(out=warm[:], in_=shift[:, 0:1], func=ACT.Silu)
+                keep_bias(GROUPS - 1)
             if 1 <= step <= GROUPS:
                 g = step - 1
                 eg = work.tile([P, P, 4], BF16, name="eg", align_bytes=64)
-                nc.vector.tensor_tensor(out=eg[:], in0=xs[g][:], in1=cts[g][:], op=ALU.mult)
+                nc.vector.tensor_tensor(out=eg[:], in0=xs[g][:].rearrange("p j b -> p b j"), in1=cts[g][:], op=ALU.mult)
                 egs[g] = eg
             if step >= 2:
                 g = step - 2
                 nc.vector.quantize_mx(out=embq[:, g, :].bitcast(FP8X4), scales=embs[:, g, :],
                                       in_=egs[g][:].rearrange("p b j -> p (b j)"))
-                spread_bias(2 * g)
-                spread_bias(2 * g + 1)
+                if g == 2:
+                    spread_bias(GROUPS - 1, accp, "acc3")
                 layer1_passes(g, (0, 1, 2))
+
+        def h_bank(c):
+            z = work.tile([P, 4, P], F32, name="z", bufs=3)
+            nc.vector.tensor_tensor(out=z[:], in0=acc1[c][:].rearrange("p (q t) -> p t q", t=4), in1=b1s[:, c], op=ALU.add)
+            xt = auxp.tile([P, NT], F32, name="aux%d" % (c % 2))
+            for j in range(4):
+                nc.tensor.transpose(xt[:, j * P:(j + 1) * P], z[:, j, :], ident_f[:])
+            hg = work.tile([P, P, 4], BF16, name="hg", bufs=3, align_bytes=64)
+            nc.scalar.activation(out=hg[:], in_=xt[:].rearrange("p (t r) -> p r t", t=4), func=ACT.Silu)
+            return hg
+
+        def quantize_h(c, hg):
+            nc.vector.quantize_mx(out=hq[:, c, :].bitcast(FP8X4), scales=hs[:, c, :], in_=hg[:].rearrange("p b j -> p (b j)"))
 
         for c in range(3, BANKS):
             acc1[c] = accp.tile([P, NT], F32, name="acc%d" % c)
-        layer1_passes(0, (3, 4, 5))
-        layer1_passes(1, (3, 4, 5))
-        h_banks((0, 1, 2))
-        for g in range(2, GROUPS):
+        hgs = {}
+        for c in range(3):
+            layer1_passes(c, (3, 4, 5))
+            hgs[c] = h_bank(c)
+        for c in range(3):
+            quantize_h(c, hgs[c])
+        for g in range(3, GROUPS):
+            for k in (2 * g, 2 * g + 1):
+                spread_bias(k, auxp, "aux%d" % (k % 2))
+                keep_bias(k)
             layer1_passes(g, (3, 4, 5))
-        h_banks((3, 4, 5))
+        for c in range(3, BANKS):
+            hgs[c] = h_bank(c)
+        for c in range(3, BANKS):
+            quantize_h(c, hgs[c])
 
         acc2 = [accp.tile([P, NT], F32, name="acc%d" % c) for c in range(BANKS)]
-        for g in range(GROUPS - 1):
+
+        def layer2_pass(c, g, words):
             pi, k = w2_plane(g)
+            nc.tensor.matmul_mx(out=acc2[c][:], lhsT=hq[:, g, :].bitcast(FP8X4), lhsT_scale=hs[:, g, :],
+                                rhs=words.bitcast(FP8X4), rhs_scale=planes[pi][k:P, c * NT:(c + 1) * NT],
+                                start=(g == 0), stop=(g == GROUPS - 1))
+
+        for g in range(GROUPS - 1):
             for c in range(BANKS):
-                cols = slice(c * NT, (c + 1) * NT)
-                nc.tensor.matmul_mx(out=acc2[c][:], lhsT=hq[:, g, :].bitcast(FP8X4), lhsT_scale=hs[:, g, :],
-                                    rhs=w2[g][:, cols].bitcast(FP8X4), rhs_scale=planes[pi][k:P, cols],
-                                    start=(g == 0), stop=False)
-        g = GROUPS - 1
-        pi, k = w2_plane(g)
+                layer2_pass(c, g, w2[g][:, c * NT:(c + 1) * NT])
         for c in range(BANKS):
             cols = slice(c * NT, (c + 1) * NT)
-            nc.tensor.matmul_mx(out=acc2[c][:], lhsT=hq[:, g, :].bitcast(FP8X4), lhsT_scale=hs[:, g, :],
-                                rhs=w2last[c][:].bitcast(FP8X4), rhs_scale=planes[pi][k:P, cols],
-                                start=False, stop=True)
+            layer2_pass(c, GROUPS - 1, w2last[c][:])
             z2 = work.tile([P, NT], F32, name="z2", bufs=3)
             nc.vector.tensor_tensor(out=z2[:], in0=acc2[c][:], in1=b2b[:, cols], op=ALU.add)
             o = work.tile([P, NT], F32, name="o", bufs=6)

@@ -22,12 +22,16 @@ BANKS = 6
 FLOPS = 2 * 2 * 128 * 3072 * 3072
 
 
+LAST_LOADS = [(0, 1024), (1024, 1024), (2048, 512), (2560, 256), (2816, 256)]
+OUT_PIECES = [(0, 512), (512, 512), (1024, 512), (1536, 512), (2048, 512), (2560, 256), (2816, 256)]
+
+
 def w1_plane(g):
-    return (g // 4, 4 * (g % 4))
+    return (0, 4 * g) if g < 4 else (1, 4 * (g - 4))
 
 
 def w2_plane(g):
-    return ((g + GROUPS) // 4, 4 * ((g + GROUPS) % 4))
+    return (2, 4 * g) if g < 4 else (3, 4 * (g - 2))
 
 
 def tile_input_timestep_w_kernel(tc, t, W1_words, W1_scales, b1, W2_words, W2_scales, b2, out):
@@ -40,7 +44,7 @@ def tile_input_timestep_w_kernel(tc, t, W1_words, W1_scales, b1, W2_words, W2_sc
         accp = ctx.enter_context(tc.psum_pool(name="acc", bufs=1))
         auxp = ctx.enter_context(tc.psum_pool(name="aux", bufs=1))
 
-        planes = [const.tile([P, WIDTH], U8, name="plane%d" % i, align_bytes=64) for i in range(3)]
+        planes = [const.tile([P, WIDTH], U8, name="plane%d" % i, align_bytes=256) for i in range(4)]
         trow = const.tile([P, P], BF16, name="trow")
         rows = const.tile([P, NT], BF16, name="rows")
         ident_b = const.tile([P, P], BF16, name="ident_b")
@@ -59,23 +63,24 @@ def tile_input_timestep_w_kernel(tc, t, W1_words, W1_scales, b1, W2_words, W2_sc
         embs = const.tile([P, GROUPS, P], U8, name="embs", align_bytes=64)
         hq = const.tile([P, GROUPS, P], U32, name="hq", align_bytes=64)
         hs = const.tile([P, GROUPS, P], U8, name="hs", align_bytes=64)
-        w1 = [[wpool.tile([P, HALF], U32, name="w1_%d_%d" % (s, g), align_bytes=64) for g in range(GROUPS)]
+        w1 = [[wpool.tile([P, HALF], U32, name="w1_%d_%d" % (s, g), align_bytes=256) for g in range(GROUPS)]
               for s in range(2)]
-        w2 = [wpool.tile([P, WIDTH], U32, name="w2_%d" % g, align_bytes=64) for g in range(GROUPS - 1)]
-        w2last = [wpool.tile([P, NT], U32, name="w2l_%d" % c, align_bytes=64) for c in range(BANKS)]
+        w2 = [wpool.tile([P, WIDTH], U32, name="w2_%d" % g, align_bytes=256) for g in range(GROUPS - 1)]
+        w2last = [wpool.tile([P, w], U32, name="w2l_%d" % c, align_bytes=256) for (c, w) in LAST_LOADS]
 
         nc.vector.memset(trow[:], 0.0)
         nc.vector.memset(planes[0][:].bitcast(I32), 0)
-        nc.vector.memset(rows[:], 0.0)
         nc.vector.memset(planes[1][:].bitcast(I32), 0)
+        nc.vector.memset(rows[:], 0.0)
         nc.vector.memset(planes[2][:].bitcast(I32), 0)
+        nc.vector.memset(planes[3][:].bitcast(I32), 0)
 
         def load_planes(queue, dtype, quadrants, tile, k, scales, g, n):
             for q in quadrants:
                 queue.dma_start(out=planes[tile][32 * q + k:32 * q + k + 4 * n, :].bitcast(dtype),
                                 in_=scales[g:g + n, 4 * q:4 * q + 4, :].bitcast(dtype))
 
-        plane_loads = [(0, 0, W1_scales, 0, 4), (1, 0, W1_scales, 4, 2), (1, 8, W2_scales, 0, 2), (2, 0, W2_scales, 2, 4)]
+        plane_loads = [(0, 0, W1_scales, 0, 4), (1, 0, W1_scales, 4, 2), (2, 0, W2_scales, 0, 4), (3, 8, W2_scales, 4, 2)]
 
         def load_words(tile, words, c, w):
             nc.sync.dma_start(out=tile[:].bitcast(I32),
@@ -91,8 +96,8 @@ def tile_input_timestep_w_kernel(tc, t, W1_words, W1_scales, b1, W2_words, W2_sc
                     load_planes(nc.sync, I32, (0, 1), *plane_loads[g])
         for g in range(GROUPS - 1):
             load_words(w2[g], W2_words[g], 0, WIDTH)
-        for c in range(BANKS):
-            load_words(w2last[c], W2_words[GROUPS - 1], c * NT, NT)
+        for i, (c, w) in enumerate(LAST_LOADS):
+            load_words(w2last[i], W2_words[GROUPS - 1], c, w)
 
         make_identity(nc, ident_b[:])
         nc.gpsimd.iota(idx[:], pattern=[[NT, GROUPS], [1, 4]], base=0, channel_multiplier=4)
@@ -119,11 +124,16 @@ def tile_input_timestep_w_kernel(tc, t, W1_words, W1_scales, b1, W2_words, W2_sc
             spread[k] = pool.tile([P, NT], F32, name=bank)
             nc.tensor.matmul(spread[k][:], lhsT=ident_b[:, k:k + 1].to_broadcast([P, P]), rhs=rows[:], start=True, stop=True)
 
-        def keep_bias(k):
-            if k < GROUPS:
-                nc.scalar.copy(out=b1s[:, k], in_=spread[k][:].rearrange("p (q t) -> p t q", t=4))
+        def keep_b1(k):
+            nc.scalar.copy(out=b1s[:, k], in_=spread[k][:].rearrange("p (q t) -> p t q", t=4))
+
+        def keep_b2(k):
+            c = k - GROUPS
+            cols = slice(c * NT, (c + 1) * NT)
+            if c % 2 == 0:
+                nc.vector.tensor_copy(out=b2b[:, cols], in_=spread[k][:])
             else:
-                nc.scalar.copy(out=b2b[:, (k - GROUPS) * NT:(k - GROUPS + 1) * NT], in_=spread[k][:])
+                nc.scalar.copy(out=b2b[:, cols], in_=spread[k][:])
 
         acc1 = {}
 
@@ -135,7 +145,8 @@ def tile_input_timestep_w_kernel(tc, t, W1_words, W1_scales, b1, W2_words, W2_sc
                                     rhs_scale=planes[pi][k:P, c * NT:(c + 1) * NT],
                                     start=(g == 0), stop=(g == GROUPS - 1))
 
-        for k, (pool, bank) in enumerate([(accp, "acc3"), (accp, "acc4"), (accp, "acc5"), (auxp, "aux0"), (auxp, "aux1")]):
+        free_banks = [(accp, "acc3"), (accp, "acc4"), (accp, "acc5"), (auxp, "aux0"), (auxp, "aux1")]
+        for k, (pool, bank) in enumerate(free_banks):
             spread_bias(k, pool, bank)
         for c in range(3):
             acc1[c] = accp.tile([P, NT], F32, name="acc%d" % c)
@@ -152,7 +163,7 @@ def tile_input_timestep_w_kernel(tc, t, W1_words, W1_scales, b1, W2_words, W2_sc
                     nc.scalar.activation(out=x[:, j, :], in_=tbs[:], func=ACT.Sin,
                                          bias=shift[:, m:m + 1], scale=slope[:, m:m + 1])
                 if g >= 1:
-                    keep_bias(g - 1)
+                    keep_b1(g - 1)
                 ct = work.tile([P, P, 4], F32, name="ct")
                 nc.vector.tensor_tensor(out=ct[:], in0=tbs[:].unsqueeze(2).to_broadcast([P, P, 4]),
                                         in1=cfac2[:, 4 * g:4 * g + 4].unsqueeze(1).to_broadcast([P, P, 4]), op=ALU.mult)
@@ -160,7 +171,7 @@ def tile_input_timestep_w_kernel(tc, t, W1_words, W1_scales, b1, W2_words, W2_sc
                 cts[g] = ct
             if step == GROUPS:
                 nc.scalar.activation(out=warm[:], in_=shift[:, 0:1], func=ACT.Silu)
-                keep_bias(GROUPS - 1)
+                keep_b1(GROUPS - 1)
             if 1 <= step <= GROUPS:
                 g = step - 1
                 eg = work.tile([P, P, 4], BF16, name="eg", align_bytes=64)
@@ -173,6 +184,11 @@ def tile_input_timestep_w_kernel(tc, t, W1_words, W1_scales, b1, W2_words, W2_sc
                 if g == 2:
                     spread_bias(GROUPS - 1, accp, "acc3")
                 layer1_passes(g, (0, 1, 2))
+                if g == GROUPS - 2:
+                    for k, (pool, bank) in enumerate(free_banks):
+                        spread_bias(GROUPS + k, pool, bank)
+        for k in range(GROUPS, 2 * GROUPS - 1):
+            keep_b2(k)
 
         def h_bank(c):
             z = work.tile([P, 4, P], F32, name="z", bufs=3)
@@ -195,32 +211,34 @@ def tile_input_timestep_w_kernel(tc, t, W1_words, W1_scales, b1, W2_words, W2_sc
             hgs[c] = h_bank(c)
         for c in range(3):
             quantize_h(c, hgs[c])
+        spread_bias(2 * GROUPS - 1, auxp, "aux1")
+        keep_b2(2 * GROUPS - 1)
         for g in range(3, GROUPS):
-            for k in (2 * g, 2 * g + 1):
-                spread_bias(k, auxp, "aux%d" % (k % 2))
-                keep_bias(k)
             layer1_passes(g, (3, 4, 5))
         for c in range(3, BANKS):
             hgs[c] = h_bank(c)
         for c in range(3, BANKS):
             quantize_h(c, hgs[c])
 
-        acc2 = [accp.tile([P, NT], F32, name="acc%d" % c) for c in range(BANKS)]
+        acc2 = [accp.tile([P, NT], F32, name="acc%d" % i) for i in range(BANKS)]
+        acc2.append(auxp.tile([P, NT], F32, name="aux0"))
 
-        def layer2_pass(c, g, words):
+        def layer2_pass(i, g, words):
+            c, w = OUT_PIECES[i]
             pi, k = w2_plane(g)
-            nc.tensor.matmul_mx(out=acc2[c][:], lhsT=hq[:, g, :].bitcast(FP8X4), lhsT_scale=hs[:, g, :],
-                                rhs=words.bitcast(FP8X4), rhs_scale=planes[pi][k:P, c * NT:(c + 1) * NT],
+            nc.tensor.matmul_mx(out=acc2[i][:, 0:w], lhsT=hq[:, g, :].bitcast(FP8X4), lhsT_scale=hs[:, g, :],
+                                rhs=words.bitcast(FP8X4), rhs_scale=planes[pi][k:P, c:c + w],
                                 start=(g == 0), stop=(g == GROUPS - 1))
 
         for g in range(GROUPS - 1):
-            for c in range(BANKS):
-                layer2_pass(c, g, w2[g][:, c * NT:(c + 1) * NT])
-        for c in range(BANKS):
-            cols = slice(c * NT, (c + 1) * NT)
-            layer2_pass(c, GROUPS - 1, w2last[c][:])
+            for i, (c, w) in enumerate(OUT_PIECES):
+                layer2_pass(i, g, w2[g][:, c:c + w])
+        for i, (c, w) in enumerate(OUT_PIECES):
+            for tile, (c0, w0) in zip(w2last, LAST_LOADS):
+                if c0 <= c < c0 + w0:
+                    layer2_pass(i, GROUPS - 1, tile[:, c - c0:c - c0 + w])
             z2 = work.tile([P, NT], F32, name="z2", bufs=3)
-            nc.vector.tensor_tensor(out=z2[:], in0=acc2[c][:], in1=b2b[:, cols], op=ALU.add)
-            o = work.tile([P, NT], F32, name="o", bufs=6)
-            nc.scalar.activation(out=o[:], in_=z2[:], func=ACT.Silu)
-            nc.sync.dma_start(out=out[:, cols], in_=o[:])
+            nc.vector.tensor_tensor(out=z2[:, 0:w], in0=acc2[i][:, 0:w], in1=b2b[:, c:c + w], op=ALU.add)
+            o = work.tile([P, NT], F32, name="o", bufs=7, align_bytes=256)
+            nc.scalar.activation(out=o[:, 0:w], in_=z2[:, 0:w], func=ACT.Silu)
+            nc.sync.dma_start(out=out[:, c:c + w], in_=o[:, 0:w])

@@ -22,7 +22,6 @@ BANKS = 6
 FLOPS = 2 * 2 * 128 * 3072 * 3072
 
 
-LAST_LOADS = [(0, 1024), (1024, 1024), (2048, 512), (2560, 256), (2816, 256)]
 OUT_PIECES = [(0, 512), (512, 512), (1024, 512), (1536, 512), (2048, 512), (2560, 256), (2816, 256)]
 
 
@@ -65,8 +64,9 @@ def tile_input_timestep_w_kernel(tc, t, W1_words, W1_scales, b1, W2_words, W2_sc
         hs = const.tile([P, GROUPS, P], U8, name="hs", align_bytes=64)
         w1 = [[wpool.tile([P, HALF], U32, name="w1_%d_%d" % (s, g), align_bytes=256) for g in range(GROUPS)]
               for s in range(2)]
-        w2 = [wpool.tile([P, WIDTH], U32, name="w2_%d" % g, align_bytes=256) for g in range(GROUPS - 1)]
-        w2last = [wpool.tile([P, w], U32, name="w2l_%d" % c, align_bytes=256) for (c, w) in LAST_LOADS]
+        w2 = [[wpool.tile([P, HALF], U32, name="w2_%d_%d" % (s, g), align_bytes=256) for g in range(GROUPS - 1)]
+              for s in range(2)]
+        w2last = [wpool.tile([P, w], U32, name="w2l_%d" % c, align_bytes=256) for (c, w) in OUT_PIECES]
 
         nc.vector.memset(trow[:], 0.0)
         nc.vector.memset(planes[0][:].bitcast(I32), 0)
@@ -95,8 +95,9 @@ def tile_input_timestep_w_kernel(tc, t, W1_words, W1_scales, b1, W2_words, W2_sc
                 if s == 0 and g < 4:
                     load_planes(nc.sync, I32, (0, 1), *plane_loads[g])
         for g in range(GROUPS - 1):
-            load_words(w2[g], W2_words[g], 0, WIDTH)
-        for i, (c, w) in enumerate(LAST_LOADS):
+            for s in range(2):
+                load_words(w2[s][g], W2_words[g], s * HALF, HALF)
+        for i, (c, w) in enumerate(OUT_PIECES):
             load_words(w2last[i], W2_words[GROUPS - 1], c, w)
 
         make_identity(nc, ident_b[:])
@@ -232,11 +233,9 @@ def tile_input_timestep_w_kernel(tc, t, W1_words, W1_scales, b1, W2_words, W2_sc
 
         for g in range(GROUPS - 1):
             for i, (c, w) in enumerate(OUT_PIECES):
-                layer2_pass(i, g, w2[g][:, c:c + w])
+                layer2_pass(i, g, w2[c // HALF][g][:, c % HALF:c % HALF + w])
         for i, (c, w) in enumerate(OUT_PIECES):
-            for tile, (c0, w0) in zip(w2last, LAST_LOADS):
-                if c0 <= c < c0 + w0:
-                    layer2_pass(i, GROUPS - 1, tile[:, c - c0:c - c0 + w])
+            layer2_pass(i, GROUPS - 1, w2last[i][:])
             z2 = work.tile([P, NT], F32, name="z2", bufs=3)
             nc.vector.tensor_tensor(out=z2[:, 0:w], in0=acc2[i][:, 0:w], in1=b2b[:, c:c + w], op=ALU.add)
             o = work.tile([P, NT], F32, name="o", bufs=7, align_bytes=256)

@@ -22,6 +22,7 @@ BANKS = 6
 FLOPS = 2 * 2 * 128 * 3072 * 3072
 
 
+LAST_LOADS = [(0, 1024), (1024, 1024), (2048, 512), (2560, 256), (2816, 256)]
 OUT_PIECES = [(0, 512), (512, 512), (1024, 512), (1536, 512), (2048, 512), (2560, 256), (2816, 256)]
 
 
@@ -64,9 +65,9 @@ def tile_input_timestep_w_kernel(tc, t, W1_words, W1_scales, b1, W2_words, W2_sc
         hs = const.tile([P, GROUPS, P], U8, name="hs", align_bytes=64)
         w1 = [[wpool.tile([P, HALF], U32, name="w1_%d_%d" % (s, g), align_bytes=256) for g in range(GROUPS)]
               for s in range(2)]
-        w2 = [[wpool.tile([P, HALF], U32, name="w2_%d_%d" % (s, g), align_bytes=256) for g in range(GROUPS - 1)]
+        w2 = [[wpool.tile([P, HALF], U32, name="w2_%d_%d" % (s, g), align_bytes=256) for g in range(GROUPS - 2)]
               for s in range(2)]
-        w2last = [wpool.tile([P, w], U32, name="w2l_%d" % c, align_bytes=256) for (c, w) in OUT_PIECES]
+        w2last = [[wpool.tile([P, w], U32, name="w2l_%d_%d" % (g, c), align_bytes=256) for g in range(2)] for (c, w) in LAST_LOADS]
 
         nc.vector.memset(trow[:], 0.0)
         nc.vector.memset(planes[0][:].bitcast(I32), 0)
@@ -94,11 +95,12 @@ def tile_input_timestep_w_kernel(tc, t, W1_words, W1_scales, b1, W2_words, W2_sc
                 load_words(w1[s][g], W1_words[g], s * HALF, HALF)
                 if s == 0 and g < 4:
                     load_planes(nc.sync, I32, (0, 1), *plane_loads[g])
-        for g in range(GROUPS - 1):
+        for g in range(GROUPS - 2):
             for s in range(2):
                 load_words(w2[s][g], W2_words[g], s * HALF, HALF)
-        for i, (c, w) in enumerate(OUT_PIECES):
-            load_words(w2last[i], W2_words[GROUPS - 1], c, w)
+        for tiles, (c, w) in zip(w2last, LAST_LOADS):
+            for g in range(2):
+                load_words(tiles[g], W2_words[GROUPS - 2 + g], c, w)
 
         make_identity(nc, ident_b[:])
         nc.gpsimd.iota(idx[:], pattern=[[NT, GROUPS], [1, 4]], base=0, channel_multiplier=4)
@@ -231,13 +233,17 @@ def tile_input_timestep_w_kernel(tc, t, W1_words, W1_scales, b1, W2_words, W2_sc
                                 rhs=words.bitcast(FP8X4), rhs_scale=planes[pi][k:P, c:c + w],
                                 start=(g == 0), stop=(g == GROUPS - 1))
 
-        for g in range(GROUPS - 1):
+        for g in range(GROUPS - 2):
             for i, (c, w) in enumerate(OUT_PIECES):
                 layer2_pass(i, g, w2[c // HALF][g][:, c % HALF:c % HALF + w])
-        for i, (c, w) in enumerate(OUT_PIECES):
-            layer2_pass(i, GROUPS - 1, w2last[i][:])
-            z2 = work.tile([P, NT], F32, name="z2", bufs=3)
-            nc.vector.tensor_tensor(out=z2[:, 0:w], in0=acc2[i][:, 0:w], in1=b2b[:, c:c + w], op=ALU.add)
-            o = work.tile([P, NT], F32, name="o", bufs=7, align_bytes=256)
-            nc.scalar.activation(out=o[:, 0:w], in_=z2[:, 0:w], func=ACT.Silu)
-            nc.sync.dma_start(out=out[:, c:c + w], in_=o[:, 0:w])
+        for tiles, (c0, w0) in zip(w2last, LAST_LOADS):
+            pieces = [(i, c, w) for i, (c, w) in enumerate(OUT_PIECES) if c0 <= c < c0 + w0]
+            for i, c, w in pieces:
+                layer2_pass(i, GROUPS - 2, tiles[0][:, c - c0:c - c0 + w])
+            for i, c, w in pieces:
+                layer2_pass(i, GROUPS - 1, tiles[1][:, c - c0:c - c0 + w])
+                z2 = work.tile([P, NT], F32, name="z2", bufs=3)
+                nc.vector.tensor_tensor(out=z2[:, 0:w], in0=acc2[i][:, 0:w], in1=b2b[:, c:c + w], op=ALU.add)
+                o = work.tile([P, NT], F32, name="o", bufs=7, align_bytes=256)
+                nc.scalar.activation(out=o[:, 0:w], in_=z2[:, 0:w], func=ACT.Silu)
+                nc.sync.dma_start(out=out[:, c:c + w], in_=o[:, 0:w])

import math
from contextlib import ExitStack

import concourse.mybir as mybir
from concourse.masks import make_identity

F32 = mybir.dt.float32
BF16 = mybir.dt.bfloat16
I32 = mybir.dt.int32
U32 = mybir.dt.uint32
U8 = mybir.dt.uint8
FP8X4 = mybir.dt.float8_e4m3fn_x4
ALU = mybir.AluOpType
ACT = mybir.ActivationFunctionType

P = 128
WIDTH = 3072
HALF = 1536
GROUPS = 6
NT = 512
BANKS = 6
FLOPS = 2 * 2 * 128 * 3072 * 3072


LAST_LOADS = [(0, 1024), (1024, 1024), (2048, 512), (2560, 256), (2816, 256)]
OUT_PIECES = [(0, 512), (512, 512), (1024, 512), (1536, 512), (2048, 512), (2560, 256), (2816, 256)]


def w1_plane(g):
    return (0, 4 * g) if g < 4 else (1, 4 * (g - 4))


def w2_plane(g):
    return (2, 4 * g) if g < 4 else (3, 4 * (g - 2))


def tile_input_timestep_w_kernel(tc, t, W1_words, W1_scales, b1, W2_words, W2_scales, b2, out):
    nc = tc.nc
    with ExitStack() as ctx:
        ctx.enter_context(tc.manual_schedule())
        const = ctx.enter_context(tc.tile_pool(name="const", bufs=1))
        wpool = ctx.enter_context(tc.tile_pool(name="weights", bufs=1))
        work = ctx.enter_context(tc.tile_pool(name="work", bufs=2))
        accp = ctx.enter_context(tc.psum_pool(name="acc", bufs=1))
        auxp = ctx.enter_context(tc.psum_pool(name="aux", bufs=1))

        planes = [const.tile([P, WIDTH], U8, name="plane%d" % i, align_bytes=256) for i in range(4)]
        trow = const.tile([P, P], BF16, name="trow")
        rows = const.tile([P, NT], BF16, name="rows")
        ident_b = const.tile([P, P], BF16, name="ident_b")
        ident_f = const.tile([P, P], F32, name="ident_f")
        idx = const.tile([P, 4 * GROUPS], I32, name="idx")
        idxf = const.tile([P, 4 * GROUPS], F32, name="idxf")
        slope = const.tile([P, 4 * GROUPS], F32, name="slope")
        shift = const.tile([P, 4 * GROUPS], F32, name="shift")
        cfac = const.tile([P, 4 * GROUPS], F32, name="cfac")
        cfac2 = const.tile([P, 4 * GROUPS], F32, name="cfac2")
        warm = const.tile([P, 1], F32, name="warm")
        tbs = const.tile([P, P], F32, name="tbs")
        b1s = const.tile([P, GROUPS, 4, P], BF16, name="b1s")
        b2b = const.tile([P, WIDTH], BF16, name="b2b")
        embq = const.tile([P, GROUPS, P], U32, name="embq", align_bytes=64)
        embs = const.tile([P, GROUPS, P], U8, name="embs", align_bytes=64)
        hq = const.tile([P, GROUPS, P], U32, name="hq", align_bytes=64)
        hs = const.tile([P, GROUPS, P], U8, name="hs", align_bytes=64)
        w1 = [[wpool.tile([P, HALF], U32, name="w1_%d_%d" % (s, g), align_bytes=256) for g in range(GROUPS)]
              for s in range(2)]
        w2 = [[wpool.tile([P, HALF], U32, name="w2_%d_%d" % (s, g), align_bytes=256) for g in range(GROUPS - 2)]
              for s in range(2)]
        w2last = [[wpool.tile([P, w], U32, name="w2l_%d_%d" % (g, c), align_bytes=256) for g in range(2)] for (c, w) in LAST_LOADS]

        nc.vector.memset(trow[:], 0.0)
        nc.vector.memset(planes[0][:].bitcast(I32), 0)
        nc.vector.memset(planes[1][:].bitcast(I32), 0)
        nc.vector.memset(rows[:], 0.0)
        nc.vector.memset(planes[2][:].bitcast(I32), 0)
        nc.vector.memset(planes[3][:].bitcast(I32), 0)

        def load_planes(queue, dtype, quadrants, tile, k, scales, g, n):
            for q in quadrants:
                queue.dma_start(out=planes[tile][32 * q + k:32 * q + k + 4 * n, :].bitcast(dtype),
                                in_=scales[g:g + n, 4 * q:4 * q + 4, :].bitcast(dtype))

        plane_loads = [(0, 0, W1_scales, 0, 4), (1, 0, W1_scales, 4, 2), (2, 0, W2_scales, 0, 4), (3, 8, W2_scales, 4, 2)]

        def load_words(tile, words, c, w):
            nc.sync.dma_start(out=tile[:].bitcast(I32),
                              in_=words.rearrange("p n t -> p (n t)")[:, 4 * c:4 * (c + w)].bitcast(I32))

        nc.scalar.dma_start(out=trow[0:1, :], in_=t.rearrange("(o n) -> o n", o=1))
        nc.scalar.dma_start(out=rows[0:6, :], in_=b1.rearrange("(c n) -> c n", c=6))
        nc.scalar.dma_start(out=rows[6:12, :], in_=b2.rearrange("(c n) -> c n", c=6))
        for s in range(2):
            for g in range(GROUPS):
                load_words(w1[s][g], W1_words[g], s * HALF, HALF)
                if s == 0 and g < 4:
                    load_planes(nc.sync, I32, (0, 1), *plane_loads[g])
        for g in range(GROUPS - 2):
            for s in range(2):
                load_words(w2[s][g], W2_words[g], s * HALF, HALF)
        for tiles, (c, w) in zip(w2last, LAST_LOADS):
            for g in range(2):
                load_words(tiles[g], W2_words[GROUPS - 2 + g], c, w)

        make_identity(nc, ident_b[:])
        nc.gpsimd.iota(idx[:], pattern=[[NT, GROUPS], [1, 4]], base=0, channel_multiplier=4)
        load_planes(nc.gpsimd, F32, (2, 3), *plane_loads[0])
        load_planes(nc.gpsimd, F32, (2, 3), *plane_loads[1])
        make_identity(nc, ident_f[:])
        load_planes(nc.gpsimd, F32, (2, 3), *plane_loads[2])
        load_planes(nc.gpsimd, F32, (2, 3), *plane_loads[3])

        nc.vector.tensor_copy(out=idxf[:], in_=idx[:])
        nc.vector.tensor_scalar_mul(out=slope[:], in0=idxf[:], scalar1=-math.pi / WIDTH)
        nc.vector.tensor_scalar(out=shift[:], in0=idxf[:], scalar1=math.pi / (2 * WIDTH), scalar2=math.pi / 4,
                                op0=ALU.mult, op1=ALU.add)
        nc.scalar.activation(out=cfac[:], in_=shift[:], func=ACT.Sin)
        nc.vector.tensor_scalar_mul(out=cfac2[:], in0=cfac[:], scalar1=2.0)

        tb = auxp.tile([P, NT], F32, name="aux1")
        nc.tensor.matmul(tb[:, 0:P], lhsT=ident_b[:, 0:1].to_broadcast([P, P]), rhs=trow[:], start=True, stop=True)
        nc.scalar.copy(out=tbs[:], in_=tb[:, 0:P])

        spread = {}

        def spread_bias(k, pool, bank):
            spread[k] = pool.tile([P, NT], F32, name=bank)
            nc.tensor.matmul(spread[k][:], lhsT=ident_b[:, k:k + 1].to_broadcast([P, P]), rhs=rows[:], start=True, stop=True)

        def keep_b1(k):
            nc.scalar.copy(out=b1s[:, k], in_=spread[k][:].rearrange("p (q t) -> p t q", t=4))

        def keep_b2(k):
            c = k - GROUPS
            cols = slice(c * NT, (c + 1) * NT)
            if c % 2 == 0:
                nc.vector.tensor_copy(out=b2b[:, cols], in_=spread[k][:])
            else:
                nc.scalar.copy(out=b2b[:, cols], in_=spread[k][:])

        acc1 = {}

        def layer1_passes(g, banks):
            pi, k = w1_plane(g)
            for c in banks:
                nc.tensor.matmul_mx(out=acc1[c][:], lhsT=embq[:, g, :].bitcast(FP8X4), lhsT_scale=embs[:, g, :],
                                    rhs=w1[c // 3][g][:, (c % 3) * NT:(c % 3 + 1) * NT].bitcast(FP8X4),
                                    rhs_scale=planes[pi][k:P, c * NT:(c + 1) * NT],
                                    start=(g == 0), stop=(g == GROUPS - 1))

        free_banks = [(accp, "acc3"), (accp, "acc4"), (accp, "acc5"), (auxp, "aux0"), (auxp, "aux1")]
        for k, (pool, bank) in enumerate(free_banks):
            spread_bias(k, pool, bank)
        for c in range(3):
            acc1[c] = accp.tile([P, NT], F32, name="acc%d" % c)

        xs = {}
        cts = {}
        egs = {}
        for step in range(GROUPS + 2):
            if step < GROUPS:
                g = step
                x = work.tile([P, 4, P], F32, name="x", bufs=3)
                for j in range(4):
                    m = 4 * g + j
                    nc.scalar.activation(out=x[:, j, :], in_=tbs[:], func=ACT.Sin,
                                         bias=shift[:, m:m + 1], scale=slope[:, m:m + 1])
                if g >= 1:
                    keep_b1(g - 1)
                ct = work.tile([P, P, 4], F32, name="ct")
                nc.vector.tensor_tensor(out=ct[:], in0=tbs[:].unsqueeze(2).to_broadcast([P, P, 4]),
                                        in1=cfac2[:, 4 * g:4 * g + 4].unsqueeze(1).to_broadcast([P, P, 4]), op=ALU.mult)
                xs[g] = x
                cts[g] = ct
            if step == GROUPS:
                nc.scalar.activation(out=warm[:], in_=shift[:, 0:1], func=ACT.Silu)
                keep_b1(GROUPS - 1)
            if 1 <= step <= GROUPS:
                g = step - 1
                eg = work.tile([P, P, 4], BF16, name="eg", align_bytes=64)
                nc.vector.tensor_tensor(out=eg[:], in0=xs[g][:].rearrange("p j b -> p b j"), in1=cts[g][:], op=ALU.mult)
                egs[g] = eg
            if step >= 2:
                g = step - 2
                nc.vector.quantize_mx(out=embq[:, g, :].bitcast(FP8X4), scales=embs[:, g, :],
                                      in_=egs[g][:].rearrange("p b j -> p (b j)"))
                if g == 2:
                    spread_bias(GROUPS - 1, accp, "acc3")
                layer1_passes(g, (0, 1, 2))
                if g == GROUPS - 2:
                    for k, (pool, bank) in enumerate(free_banks):
                        spread_bias(GROUPS + k, pool, bank)
        for k in range(GROUPS, 2 * GROUPS - 1):
            keep_b2(k)

        def h_bank(c):
            z = work.tile([P, 4, P], F32, name="z", bufs=3)
            nc.vector.tensor_tensor(out=z[:], in0=acc1[c][:].rearrange("p (q t) -> p t q", t=4), in1=b1s[:, c], op=ALU.add)
            xt = auxp.tile([P, NT], F32, name="aux%d" % (c % 2))
            for j in range(4):
                nc.tensor.transpose(xt[:, j * P:(j + 1) * P], z[:, j, :], ident_f[:])
            hg = work.tile([P, P, 4], BF16, name="hg", bufs=3, align_bytes=64)
            nc.scalar.activation(out=hg[:], in_=xt[:].rearrange("p (t r) -> p r t", t=4), func=ACT.Silu)
            return hg

        def quantize_h(c, hg):
            nc.vector.quantize_mx(out=hq[:, c, :].bitcast(FP8X4), scales=hs[:, c, :], in_=hg[:].rearrange("p b j -> p (b j)"))

        for c in range(3, BANKS):
            acc1[c] = accp.tile([P, NT], F32, name="acc%d" % c)
        hgs = {}
        for c in range(3):
            layer1_passes(c, (3, 4, 5))
            hgs[c] = h_bank(c)
        for c in range(3):
            quantize_h(c, hgs[c])
        spread_bias(2 * GROUPS - 1, auxp, "aux1")
        keep_b2(2 * GROUPS - 1)
        for g in range(3, GROUPS):
            layer1_passes(g, (3, 4, 5))
        for c in range(3, BANKS):
            hgs[c] = h_bank(c)
        for c in range(3, BANKS):
            quantize_h(c, hgs[c])

        acc2 = [accp.tile([P, NT], F32, name="acc%d" % i) for i in range(BANKS)]
        acc2.append(auxp.tile([P, NT], F32, name="aux0"))

        def layer2_pass(i, g, words):
            c, w = OUT_PIECES[i]
            pi, k = w2_plane(g)
            nc.tensor.matmul_mx(out=acc2[i][:, 0:w], lhsT=hq[:, g, :].bitcast(FP8X4), lhsT_scale=hs[:, g, :],
                                rhs=words.bitcast(FP8X4), rhs_scale=planes[pi][k:P, c:c + w],
                                start=(g == 0), stop=(g == GROUPS - 1))

        for g in range(GROUPS - 2):
            for i, (c, w) in enumerate(OUT_PIECES):
                layer2_pass(i, g, w2[c // HALF][g][:, c % HALF:c % HALF + w])
        for tiles, (c0, w0) in zip(w2last, LAST_LOADS):
            pieces = [(i, c, w) for i, (c, w) in enumerate(OUT_PIECES) if c0 <= c < c0 + w0]
            for i, c, w in pieces:
                layer2_pass(i, GROUPS - 2, tiles[0][:, c - c0:c - c0 + w])
            for i, c, w in pieces:
                layer2_pass(i, GROUPS - 1, tiles[1][:, c - c0:c - c0 + w])
                z2 = work.tile([P, NT], F32, name="z2", bufs=3)
                nc.vector.tensor_tensor(out=z2[:, 0:w], in0=acc2[i][:, 0:w], in1=b2b[:, c:c + w], op=ALU.add)
                o = work.tile([P, NT], F32, name="o", bufs=7, align_bytes=256)
                nc.scalar.activation(out=o[:, 0:w], in_=z2[:, 0:w], func=ACT.Silu)
                nc.sync.dma_start(out=out[:, c:c + w], in_=o[:, 0:w])
